import numpy as np
import ml_dtypes


def mxq(x, axis, fmt="e4m3"):
    dtype, down = {"e4m3": (ml_dtypes.float8_e4m3fn, 7), "e5m2": (ml_dtypes.float8_e5m2, 14)}[fmt]
    v = np.moveaxis(np.asarray(x, np.float32).astype(ml_dtypes.bfloat16).astype(np.float64), axis, -1)
    blocks = v.reshape(v.shape[:-1] + (-1, 32))
    amax = np.abs(blocks).max(-1, keepdims=True)
    byte = np.maximum(np.where(amax > 0, np.frexp(amax)[1] - 1 + 127, 0) - down, 1)
    scale = np.exp2(byte - 127.0)
    codes = (blocks / scale).astype(np.float32).astype(dtype).astype(np.float64)
    return np.moveaxis((codes * scale).reshape(v.shape), -1, axis)


WIDE = False


def mx_kscale(k):
    if not WIDE:
        return np.ones(k)
    levels = np.array([10, -10, 5, -5, 0])
    a = np.random.permutation(np.resize(levels, k // 512 * 4)).reshape(k // 512, 4)
    idx = np.arange(k)
    return np.exp2(a[idx // 512, idx % 128 // 32])


BF16 = ml_dtypes.bfloat16


def bf(x):
    return np.asarray(x, np.float32).astype(BF16)


def f64(x):
    return np.asarray(x).astype(np.float64)


N, K, H = 8192, 2, 256


def sigmoid(v):
    return 1.0 / (1.0 + np.exp(-v))


def setup_inputs():
    s = mx_kscale(2 * H)[:H]
    s2 = np.concatenate([s, s])
    w = 1.0 / np.sqrt(H * (K + 2))
    return {"mailbox_h": bf(np.random.standard_normal((N, K, H)) * s),
            "mailbox_c": bf(np.random.standard_normal((N, K, H)) / np.sqrt(K)),
            "U_iou_w": bf(np.random.standard_normal((3 * H, 2 * H)) * w / s2),
            "b_iou": bf(np.random.standard_normal((1, 3 * H)) * 0.1),
            "U_f_w": bf(np.random.standard_normal((H, 2 * H)) * w / s2),
            "U_f_b": bf(np.random.standard_normal(H) * 0.1)}


def reference(mailbox_h, mailbox_c, U_iou_w, b_iou, U_f_w, U_f_b):
    mh = f64(mailbox_h)
    mc = f64(mailbox_c)
    h_cat = mh.sum(axis=1)
    h_max = mh.max(axis=1)
    h_combined = np.concatenate([h_cat, h_max], axis=1)
    hq = mxq(h_combined, 1, "e4m3")
    f = sigmoid((hq @ mxq(f64(U_f_w), 1, "e4m3").T) + f64(U_f_b))
    c_agg = np.sum(f[:, None, :] * mc, axis=1)
    iou = hq @ mxq(f64(U_iou_w), 1, "e4m3").T
    iou = iou + f64(b_iou)
    i, o, u = np.split(iou, 3, axis=1)
    c = sigmoid(i) * np.tanh(u) + c_agg
    h = sigmoid(o) * np.tanh(c)
    return np.concatenate([h, c], axis=1)

@@ -1,0 +1,197 @@
+from contextlib import ExitStack
+
+import concourse.mybir as mybir
+from concourse.masks import make_identity
+
+F32 = mybir.dt.float32
+BF16 = mybir.dt.bfloat16
+U32 = mybir.dt.uint32
+U8 = mybir.dt.uint8
+FP8X4 = mybir.dt.float8_e4m3fn_x4
+ACT = mybir.ActivationFunctionType
+ALU = mybir.AluOpType
+
+P = 128
+PACK = 4
+NODES = 8192
+CHILDREN = 2
+HID = 256
+K_IN = 2 * HID
+GROUP = 512
+TILES = GROUP // P
+N_GROUPS = NODES // GROUP
+HALVES = HID // P
+PAIR_NODES = P // CHILDREN
+PAIR_TILES = GROUP // PAIR_NODES
+W_TILES = 4 * HALVES
+GATE_I, GATE_O, GATE_U, GATE_F = 0 * HALVES, 1 * HALVES, 2 * HALVES, 3 * HALVES
+
+FLOPS = 2 * NODES * K_IN * 4 * HID
+
+
+def k_onto_partitions(nc, psum_turn, rows, ident_bf, grouped):
+    turned = psum_turn.tile([P, PACK, 2 * P], BF16, tag="turned")
+    for half in range(2):
+        for t in range(PACK):
+            nc.tensor.transpose(
+                turned[:, t, half * P : (half + 1) * P],
+                rows[:, half, t * P : (t + 1) * P],
+                ident_bf[:],
+            )
+    nc.scalar.copy(out=grouped, in_=turned[:].rearrange("p t r -> p r t"))
+
+
+def tile_treelstmcellv2_t_kernel(
+    tc, mailbox_h, mailbox_c, U_iou_w, b_iou, U_f_w, U_f_b, out
+):
+    nc = tc.nc
+    h_view = mailbox_h.rearrange("(g j p) k f -> g p j k f", j=TILES, p=P)
+    out_view = out.rearrange("(g j p) c -> g p j c", j=TILES, p=P)
+    c_view = mailbox_c.rearrange("n k f -> (n k) f").rearrange(
+        "(g r p) f -> g p r f", r=PAIR_TILES, p=P
+    )
+
+    with ExitStack() as ctx:
+        const = ctx.enter_context(tc.tile_pool(name="const", bufs=1))
+        loads = ctx.enter_context(tc.tile_pool(name="loads", bufs=3))
+        quant = ctx.enter_context(tc.tile_pool(name="quant", bufs=2))
+        gates = ctx.enter_context(tc.tile_pool(name="gates", bufs=3))
+        stores = ctx.enter_context(tc.tile_pool(name="stores", bufs=3))
+        psum_turn = ctx.enter_context(tc.psum_pool(name="psum_turn", bufs=2))
+        psum_gate = ctx.enter_context(tc.psum_pool(name="psum_gate", bufs=3))
+        psum_rest = ctx.enter_context(tc.psum_pool(name="psum_rest", bufs=1))
+
+        ident_bf = const.tile([P, P], BF16)
+        make_identity(nc, ident_bf[:])
+        ident_f32 = const.tile([P, P], F32)
+        make_identity(nc, ident_f32[:])
+        pair_sum = const.tile([P, PAIR_NODES], BF16)
+        ident_pairs = ident_bf[:].rearrange("p (n two) -> p two n", two=CHILDREN)
+        nc.vector.tensor_tensor(
+            out=pair_sum[:], in0=ident_pairs[:, 0, :], in1=ident_pairs[:, 1, :], op=ALU.add
+        )
+
+        w_rows = const.tile([P, W_TILES, K_IN], BF16)
+        nc.sync.dma_start(
+            out=w_rows[:, 0:GATE_F, :], in_=U_iou_w.rearrange("(m p) k -> p m k", p=P)
+        )
+        nc.sync.dma_start(
+            out=w_rows[:, GATE_F:W_TILES, :], in_=U_f_w.rearrange("(m p) k -> p m k", p=P)
+        )
+        w_grouped = const.tile([P, W_TILES * P, PACK], BF16, align_bytes=64)
+        for m in range(0, W_TILES, 2):
+            k_onto_partitions(
+                nc, psum_turn, w_rows[:, m : m + 2, :], ident_bf,
+                w_grouped[:, m * P : (m + 2) * P, :],
+            )
+        w_codes = const.tile([P, W_TILES * P], U32, align_bytes=64)
+        w_scales = const.tile([P, W_TILES * P], U8, align_bytes=64)
+        nc.vector.quantize_mx(
+            out=w_codes[:].bitcast(FP8X4),
+            scales=w_scales[:],
+            in_=w_grouped[:].rearrange("p c t -> p (c t)"),
+        )
+
+        bias_rows = const.tile([P, P], BF16)
+        nc.vector.memset(bias_rows[:], 0.0)
+        nc.sync.dma_start(
+            out=bias_rows[0:GATE_F, :], in_=b_iou.rearrange("o (m c) -> (o m) c", c=P)
+        )
+        nc.sync.dma_start(
+            out=bias_rows[GATE_F:W_TILES, :], in_=U_f_b.rearrange("(m c) -> m c", c=P)
+        )
+        bias_turned = psum_turn.tile([P, P], BF16, tag="turned")
+        nc.tensor.transpose(bias_turned[:], bias_rows[:], ident_bf[:])
+        bias = const.tile([P, W_TILES], F32)
+        nc.vector.tensor_copy(out=bias[:], in_=bias_turned[:, 0:W_TILES])
+
+        for g in range(N_GROUPS):
+            h_rows = loads.tile([P, TILES, CHILDREN, HID], BF16)
+            nc.sync.dma_start(out=h_rows[:], in_=h_view[g])
+            c_rows = loads.tile([P, PAIR_TILES, HID], BF16)
+            nc.sync.dma_start(out=c_rows[:], in_=c_view[g])
+
+            hc = quant.tile([P, TILES, K_IN], BF16)
+            nc.vector.tensor_tensor(
+                out=hc[:, :, 0:HID], in0=h_rows[:, :, 0, :], in1=h_rows[:, :, 1, :], op=ALU.add
+            )
+            nc.vector.tensor_tensor(
+                out=hc[:, :, HID:K_IN], in0=h_rows[:, :, 0, :], in1=h_rows[:, :, 1, :], op=ALU.max
+            )
+            hc_grouped = quant.tile([P, GROUP, PACK], BF16, align_bytes=64)
+            for j in range(0, TILES, 2):
+                k_onto_partitions(
+                    nc, psum_turn, hc[:, j : j + 2, :], ident_bf,
+                    hc_grouped[:, j * P : (j + 2) * P, :],
+                )
+            hc_codes = quant.tile([P, GROUP], U32, align_bytes=64)
+            hc_scales = quant.tile([P, GROUP], U8, align_bytes=64)
+            nc.vector.quantize_mx(
+                out=hc_codes[:].bitcast(FP8X4),
+                scales=hc_scales[:],
+                in_=hc_grouped[:].rearrange("p n t -> p (n t)"),
+            )
+
+            result = stores.tile([P, TILES, 2 * HID], F32)
+            for half in range(HALVES):
+                feats = slice(half * P, (half + 1) * P)
+
+                def gate(first_tile, func, name):
+                    m = first_tile + half
+                    acc = psum_gate.tile([P, GROUP], F32, tag="acc")
+                    nc.tensor.matmul_mx(
+                        out=acc[:],
+                        lhsT=w_codes[:, m * P : (m + 1) * P].bitcast(FP8X4),
+                        lhsT_scale=w_scales[:, m * P : (m + 1) * P],
+                        rhs=hc_codes[:].bitcast(FP8X4),
+                        rhs_scale=hc_scales[:],
+                        start=True,
+                        stop=True,
+                    )
+                    value = gates.tile([P, GROUP], F32, name=name)
+                    nc.scalar.activation(
+                        out=value[:], in_=acc[:], func=func, bias=bias[:, m : m + 1], scale=1.0
+                    )
+                    return value
+
+                gate_i = gate(GATE_I, ACT.Sigmoid, "gate_i")
+                gate_u = gate(GATE_U, ACT.Tanh, "gate_u")
+                gate_f = gate(GATE_F, ACT.Sigmoid, "gate_f")
+                gate_o = gate(GATE_O, ACT.Sigmoid, "gate_o")
+
+                c_sum = psum_rest.tile([P, GROUP], F32)
+                for r in range(PAIR_TILES):
+                    nc.tensor.matmul(
+                        out=c_sum[:, r * PAIR_NODES : (r + 1) * PAIR_NODES],
+                        lhsT=c_rows[:, r, feats],
+                        rhs=pair_sum[:],
+                        start=True,
+                        stop=True,
+                    )
+
+                fresh = gates.tile([P, GROUP], F32)
+                nc.vector.tensor_tensor(out=fresh[:], in0=gate_i[:], in1=gate_u[:], op=ALU.mult)
+                kept = gates.tile([P, GROUP], F32)
+                nc.vector.tensor_tensor(out=kept[:], in0=gate_f[:], in1=c_sum[:], op=ALU.mult)
+                cell = gates.tile([P, GROUP], F32)
+                nc.vector.tensor_tensor(out=cell[:], in0=fresh[:], in1=kept[:], op=ALU.add)
+
+                cell_back = psum_rest.tile([P, TILES, P], F32)
+                gate_o_back = psum_rest.tile([P, TILES, P], F32)
+                for j in range(TILES):
+                    nc.tensor.transpose(
+                        cell_back[:, j, :], cell[:, j * P : (j + 1) * P], ident_f32[:]
+                    )
+                for j in range(TILES):
+                    nc.tensor.transpose(
+                        gate_o_back[:, j, :], gate_o[:, j * P : (j + 1) * P], ident_f32[:]
+                    )
+
+                c_out = result[:, :, HID + half * P : HID + (half + 1) * P]
+                nc.vector.tensor_copy(out=c_out, in_=cell_back[:])
+                tanh_c = gates.tile([P, TILES, P], F32)
+                nc.scalar.activation(out=tanh_c[:], in_=c_out, func=ACT.Tanh)
+                nc.vector.tensor_tensor(
+                    out=result[:, :, feats], in0=gate_o_back[:], in1=tanh_c[:], op=ALU.mult
+                )
+            nc.sync.dma_start(out=out_view[g], in_=result[:])

@@ -29,16 +29,16 @@ GATE_I, GATE_O, GATE_U, GATE_F = 0 * HALVES, 1 * HALVES, 2 * HALVES, 3 * HALVES
 FLOPS = 2 * NODES * K_IN * 4 * HID
 
 
-def k_onto_partitions(nc, psum_turn, rows, ident_bf, grouped):
-    turned = psum_turn.tile([P, PACK, 2 * P], BF16, tag="turned")
+def k_onto_partitions(nc, psum_turn, row_pairs, ident_f32, grouped_pairs):
+    turned = psum_turn.tile([P, PACK // 2, 2 * P], F32, tag="turned")
     for half in range(2):
-        for t in range(PACK):
+        for u in range(PACK // 2):
             nc.tensor.transpose(
-                turned[:, t, half * P : (half + 1) * P],
-                rows[:, half, t * P : (t + 1) * P],
-                ident_bf[:],
+                turned[:, u, half * P : (half + 1) * P],
+                row_pairs[:, half, u * P : (u + 1) * P],
+                ident_f32[:],
             )
-    nc.scalar.copy(out=grouped, in_=turned[:].rearrange("p t r -> p r t"))
+    nc.scalar.copy(out=grouped_pairs, in_=turned[:].rearrange("p u r -> p r u"))
 
 
 def tile_treelstmcellv2_t_kernel(
@@ -81,8 +81,8 @@ def tile_treelstmcellv2_t_kernel(
         w_grouped = const.tile([P, W_TILES * P, PACK], BF16, align_bytes=64)
         for m in range(0, W_TILES, 2):
             k_onto_partitions(
-                nc, psum_turn, w_rows[:, m : m + 2, :], ident_bf,
-                w_grouped[:, m * P : (m + 2) * P, :],
+                nc, psum_turn, w_rows[:].bitcast(F32)[:, m : m + 2, :], ident_f32,
+                w_grouped[:].bitcast(F32)[:, m * P : (m + 2) * P, :],
             )
         w_codes = const.tile([P, W_TILES * P], U32, align_bytes=64)
         w_scales = const.tile([P, W_TILES * P], U8, align_bytes=64)
@@ -121,8 +121,8 @@ def tile_treelstmcellv2_t_kernel(
             hc_grouped = quant.tile([P, GROUP, PACK], BF16, align_bytes=64)
             for j in range(0, TILES, 2):
                 k_onto_partitions(
-                    nc, psum_turn, hc[:, j : j + 2, :], ident_bf,
-                    hc_grouped[:, j * P : (j + 2) * P, :],
+                    nc, psum_turn, hc[:].bitcast(F32)[:, j : j + 2, :], ident_f32,
+                    hc_grouped[:].bitcast(F32)[:, j * P : (j + 2) * P, :],
                 )
             hc_codes = quant.tile([P, GROUP], U32, align_bytes=64)
             hc_scales = quant.tile([P, GROUP], U8, align_bytes=64)

@@ -21,8 +21,6 @@ GROUP = 512
 TILES = GROUP // P
 N_GROUPS = NODES // GROUP
 HALVES = HID // P
-PAIR_NODES = P // CHILDREN
-PAIR_TILES = GROUP // PAIR_NODES
 W_TILES = 4 * HALVES
 GATE_I, GATE_O, GATE_U, GATE_F = 0 * HALVES, 1 * HALVES, 2 * HALVES, 3 * HALVES
 
@@ -45,11 +43,9 @@ def tile_treelstmcellv2_t_kernel(
     tc, mailbox_h, mailbox_c, U_iou_w, b_iou, U_f_w, U_f_b, out
 ):
     nc = tc.nc
-    h_view = mailbox_h.rearrange("(g j p) k f -> g p j k f", j=TILES, p=P)
-    out_view = out.rearrange("(g j p) c -> g p j c", j=TILES, p=P)
-    c_view = mailbox_c.rearrange("n k f -> (n k) f").rearrange(
-        "(g r p) f -> g p r f", r=PAIR_TILES, p=P
-    )
+    h_view = mailbox_h.rearrange("(g p j) k f -> g p j k f", j=TILES, p=P)
+    c_view = mailbox_c.rearrange("(g p j) k f -> g p j k f", j=TILES, p=P)
+    out_view = out.rearrange("(g p j) c -> g p j c", j=TILES, p=P)
 
     with ExitStack() as ctx:
         const = ctx.enter_context(tc.tile_pool(name="const", bufs=1))
@@ -59,17 +55,12 @@ def tile_treelstmcellv2_t_kernel(
         stores = ctx.enter_context(tc.tile_pool(name="stores", bufs=3))
         psum_turn = ctx.enter_context(tc.psum_pool(name="psum_turn", bufs=2))
         psum_gate = ctx.enter_context(tc.psum_pool(name="psum_gate", bufs=3))
-        psum_rest = ctx.enter_context(tc.psum_pool(name="psum_rest", bufs=1))
+        psum_back = ctx.enter_context(tc.psum_pool(name="psum_back", bufs=1))
 
         ident_bf = const.tile([P, P], BF16)
         make_identity(nc, ident_bf[:])
         ident_f32 = const.tile([P, P], F32)
         make_identity(nc, ident_f32[:])
-        pair_sum = const.tile([P, PAIR_NODES], BF16)
-        ident_pairs = ident_bf[:].rearrange("p (n two) -> p two n", two=CHILDREN)
-        nc.vector.tensor_tensor(
-            out=pair_sum[:], in0=ident_pairs[:, 0, :], in1=ident_pairs[:, 1, :], op=ALU.add
-        )
 
         w_rows = const.tile([P, W_TILES, K_IN], BF16)
         nc.sync.dma_start(
@@ -108,8 +99,13 @@ def tile_treelstmcellv2_t_kernel(
         for g in range(N_GROUPS):
             h_rows = loads.tile([P, TILES, CHILDREN, HID], BF16)
             nc.sync.dma_start(out=h_rows[:], in_=h_view[g])
-            c_rows = loads.tile([P, PAIR_TILES, HID], BF16)
+            c_rows = loads.tile([P, TILES, CHILDREN, HID], BF16)
             nc.sync.dma_start(out=c_rows[:], in_=c_view[g])
+
+            c_sum = quant.tile([P, TILES, HID], F32)
+            nc.gpsimd.tensor_tensor(
+                out=c_sum[:], in0=c_rows[:, :, 0, :], in1=c_rows[:, :, 1, :], op=ALU.add
+            )
 
             hc = quant.tile([P, TILES, K_IN], BF16)
             nc.vector.tensor_tensor(
@@ -159,36 +155,27 @@ def tile_treelstmcellv2_t_kernel(
                 gate_f = gate(GATE_F, ACT.Sigmoid, "gate_f")
                 gate_o = gate(GATE_O, ACT.Sigmoid, "gate_o")
 
-                c_sum = psum_rest.tile([P, GROUP], F32)
-                for r in range(PAIR_TILES):
-                    nc.tensor.matmul(
-                        out=c_sum[:, r * PAIR_NODES : (r + 1) * PAIR_NODES],
-                        lhsT=c_rows[:, r, feats],
-                        rhs=pair_sum[:],
-                        start=True,
-                        stop=True,
-                    )
-
                 fresh = gates.tile([P, GROUP], F32)
                 nc.vector.tensor_tensor(out=fresh[:], in0=gate_i[:], in1=gate_u[:], op=ALU.mult)
-                kept = gates.tile([P, GROUP], F32)
-                nc.vector.tensor_tensor(out=kept[:], in0=gate_f[:], in1=c_sum[:], op=ALU.mult)
-                cell = gates.tile([P, GROUP], F32)
-                nc.vector.tensor_tensor(out=cell[:], in0=fresh[:], in1=kept[:], op=ALU.add)
 
-                cell_back = psum_rest.tile([P, TILES, P], F32)
-                gate_o_back = psum_rest.tile([P, TILES, P], F32)
-                for j in range(TILES):
-                    nc.tensor.transpose(
-                        cell_back[:, j, :], cell[:, j * P : (j + 1) * P], ident_f32[:]
-                    )
-                for j in range(TILES):
-                    nc.tensor.transpose(
-                        gate_o_back[:, j, :], gate_o[:, j * P : (j + 1) * P], ident_f32[:]
-                    )
+                def turned_back(value, name):
+                    back = psum_back.tile([P, TILES, P], F32, name=name)
+                    for j in range(TILES):
+                        nc.tensor.transpose(
+                            back[:, j, :], value[:, j * P : (j + 1) * P], ident_f32[:]
+                        )
+                    return back
 
+                gate_f_back = turned_back(gate_f, "gate_f_back")
+                fresh_back = turned_back(fresh, "fresh_back")
+                gate_o_back = turned_back(gate_o, "gate_o_back")
+
+                kept = gates.tile([P, TILES, P], F32)
+                nc.vector.tensor_tensor(
+                    out=kept[:], in0=gate_f_back[:], in1=c_sum[:, :, feats], op=ALU.mult
+                )
                 c_out = result[:, :, HID + half * P : HID + (half + 1) * P]
-                nc.vector.tensor_copy(out=c_out, in_=cell_back[:])
+                nc.vector.tensor_tensor(out=c_out, in0=fresh_back[:], in1=kept[:], op=ALU.add)
                 tanh_c = gates.tile([P, TILES, P], F32)
                 nc.scalar.activation(out=tanh_c[:], in_=c_out, func=ACT.Tanh)
                 nc.vector.tensor_tensor(

@@ -21,164 +21,272 @@ GROUP = 512
 TILES = GROUP // P
 N_GROUPS = NODES // GROUP
 HALVES = HID // P
+STEPS = N_GROUPS * HALVES
+PAIR_NODES = P // CHILDREN
+PAIR_TILES = GROUP // PAIR_NODES
+
+UNIT_TILES = 2
+UNIT_ROWS = UNIT_TILES * P
+GROUP_UNITS = GROUP // UNIT_ROWS
+HC_UNITS = N_GROUPS * GROUP_UNITS
 W_TILES = 4 * HALVES
-GATE_I, GATE_O, GATE_U, GATE_F = 0 * HALVES, 1 * HALVES, 2 * HALVES, 3 * HALVES
+W_UNITS = W_TILES // UNIT_TILES
+F_TILE = 3 * HALVES
+
+GATES = (
+    (0 * HALVES, ACT.Sigmoid),
+    (2 * HALVES, ACT.Tanh),
+    (F_TILE, ACT.Sigmoid),
+    (1 * HALVES, ACT.Sigmoid),
+)
+I, U, F, O = 0, 1, 2, 3
+LEAD = 5
+FIRST_PERIOD = 1 - LEAD - W_UNITS
+LOAD_BUFS = 4
 
 FLOPS = 2 * NODES * K_IN * 4 * HID
-
-
-def k_onto_partitions(nc, psum_turn, row_pairs, ident_f32, grouped_pairs):
-    turned = psum_turn.tile([P, PACK // 2, 2 * P], F32, tag="turned")
-    for half in range(2):
-        for u in range(PACK // 2):
-            nc.tensor.transpose(
-                turned[:, u, half * P : (half + 1) * P],
-                row_pairs[:, half, u * P : (u + 1) * P],
-                ident_f32[:],
-            )
-    nc.scalar.copy(out=grouped_pairs, in_=turned[:].rearrange("p u r -> p r u"))
 
 
 def tile_treelstmcellv2_t_kernel(
     tc, mailbox_h, mailbox_c, U_iou_w, b_iou, U_f_w, U_f_b, out
 ):
     nc = tc.nc
-    h_view = mailbox_h.rearrange("(g p j) k f -> g p j k f", j=TILES, p=P)
-    c_view = mailbox_c.rearrange("(g p j) k f -> g p j k f", j=TILES, p=P)
-    out_view = out.rearrange("(g p j) c -> g p j c", j=TILES, p=P)
+    h_view = mailbox_h.rearrange("(g j p) k f -> g p j k f", j=TILES, p=P)
+    out_view = out.rearrange("(g j p) c -> g p j c", j=TILES, p=P)
+    c_view = mailbox_c.rearrange("n k f -> (n k) f").rearrange(
+        "(g r p) f -> g p r f", r=PAIR_TILES, p=P
+    )
 
     with ExitStack() as ctx:
         const = ctx.enter_context(tc.tile_pool(name="const", bufs=1))
-        loads = ctx.enter_context(tc.tile_pool(name="loads", bufs=3))
-        quant = ctx.enter_context(tc.tile_pool(name="quant", bufs=2))
-        gates = ctx.enter_context(tc.tile_pool(name="gates", bufs=3))
+        loads = ctx.enter_context(tc.tile_pool(name="loads", bufs=LOAD_BUFS))
+        units = ctx.enter_context(tc.tile_pool(name="units", bufs=3))
+        codes = ctx.enter_context(tc.tile_pool(name="codes", bufs=4))
+        gates = ctx.enter_context(tc.tile_pool(name="gates", bufs=2))
         stores = ctx.enter_context(tc.tile_pool(name="stores", bufs=3))
-        psum_turn = ctx.enter_context(tc.psum_pool(name="psum_turn", bufs=2))
-        psum_gate = ctx.enter_context(tc.psum_pool(name="psum_gate", bufs=3))
-        psum_back = ctx.enter_context(tc.psum_pool(name="psum_back", bufs=1))
+        psum_acc = ctx.enter_context(tc.psum_pool(name="psum_acc", bufs=len(GATES)))
+        psum_rest = ctx.enter_context(tc.psum_pool(name="psum_rest", bufs=1))
+        ctx.enter_context(tc.manual_schedule())
+
+        h_rows, c_rows, unit_pairs, turned, grouped = {}, {}, {}, {}, {}
+        hc_codes, hc_scales, acc, gate, c_sum = {}, {}, {}, {}, {}
+        fresh, kept, cell_back, o_back, tanh_c, result = {}, {}, {}, {}, {}, {}
+
+        def load(g):
+            if g >= N_GROUPS:
+                return
+            h_rows[g] = loads.tile([P, TILES, CHILDREN, HID], BF16, name="h_rows")
+            nc.sync.dma_start(out=h_rows[g][:], in_=h_view[g])
+            c_rows[g] = loads.tile([P, PAIR_TILES, HID], BF16, name="c_rows")
+            nc.sync.dma_start(out=c_rows[g][:], in_=c_view[g])
+
+        bias_rows = const.tile([P, P], BF16)
+        nc.vector.memset(bias_rows[:], 0.0)
+        nc.sync.dma_start(
+            out=bias_rows[0:F_TILE, :], in_=b_iou.rearrange("o (m c) -> (o m) c", c=P)
+        )
+        nc.sync.dma_start(
+            out=bias_rows[F_TILE:W_TILES, :], in_=U_f_b.rearrange("(m c) -> m c", c=P)
+        )
+        w_rows = const.tile([P, W_TILES, K_IN], BF16)
+        nc.sync.dma_start(
+            out=w_rows[:, 0:F_TILE, :], in_=U_iou_w.rearrange("(m p) k -> p m k", p=P)
+        )
+        nc.sync.dma_start(
+            out=w_rows[:, F_TILE:W_TILES, :], in_=U_f_w.rearrange("(m p) k -> p m k", p=P)
+        )
+        for g in range(LOAD_BUFS):
+            load(g)
 
         ident_bf = const.tile([P, P], BF16)
         make_identity(nc, ident_bf[:])
         ident_f32 = const.tile([P, P], F32)
         make_identity(nc, ident_f32[:])
-
-        w_rows = const.tile([P, W_TILES, K_IN], BF16)
-        nc.sync.dma_start(
-            out=w_rows[:, 0:GATE_F, :], in_=U_iou_w.rearrange("(m p) k -> p m k", p=P)
-        )
-        nc.sync.dma_start(
-            out=w_rows[:, GATE_F:W_TILES, :], in_=U_f_w.rearrange("(m p) k -> p m k", p=P)
-        )
-        w_grouped = const.tile([P, W_TILES * P, PACK], BF16, align_bytes=64)
-        for m in range(0, W_TILES, 2):
-            k_onto_partitions(
-                nc, psum_turn, w_rows[:].bitcast(F32)[:, m : m + 2, :], ident_f32,
-                w_grouped[:].bitcast(F32)[:, m * P : (m + 2) * P, :],
-            )
-        w_codes = const.tile([P, W_TILES * P], U32, align_bytes=64)
-        w_scales = const.tile([P, W_TILES * P], U8, align_bytes=64)
-        nc.vector.quantize_mx(
-            out=w_codes[:].bitcast(FP8X4),
-            scales=w_scales[:],
-            in_=w_grouped[:].rearrange("p c t -> p (c t)"),
+        pair_sum = const.tile([P, PAIR_NODES], BF16)
+        ident_pairs = ident_bf[:].rearrange("p (n two) -> p two n", two=CHILDREN)
+        nc.vector.tensor_tensor(
+            out=pair_sum[:], in0=ident_pairs[:, 0, :], in1=ident_pairs[:, 1, :], op=ALU.add
         )
 
-        bias_rows = const.tile([P, P], BF16)
-        nc.vector.memset(bias_rows[:], 0.0)
-        nc.sync.dma_start(
-            out=bias_rows[0:GATE_F, :], in_=b_iou.rearrange("o (m c) -> (o m) c", c=P)
-        )
-        nc.sync.dma_start(
-            out=bias_rows[GATE_F:W_TILES, :], in_=U_f_b.rearrange("(m c) -> m c", c=P)
-        )
-        bias_turned = psum_turn.tile([P, P], BF16, tag="turned")
+        bias_turned = psum_rest.tile([P, P], BF16, tag="turned")
         nc.tensor.transpose(bias_turned[:], bias_rows[:], ident_bf[:])
         bias = const.tile([P, W_TILES], F32)
         nc.vector.tensor_copy(out=bias[:], in_=bias_turned[:, 0:W_TILES])
 
-        for g in range(N_GROUPS):
-            h_rows = loads.tile([P, TILES, CHILDREN, HID], BF16)
-            nc.sync.dma_start(out=h_rows[:], in_=h_view[g])
-            c_rows = loads.tile([P, TILES, CHILDREN, HID], BF16)
-            nc.sync.dma_start(out=c_rows[:], in_=c_view[g])
+        w_codes = const.tile([P, W_TILES * P], U32, align_bytes=64)
+        w_scales = const.tile([P, W_TILES * P], U8, align_bytes=64)
+        for unit in range(-W_UNITS, 0):
+            first = (unit + W_UNITS) * UNIT_TILES
+            unit_pairs[unit] = w_rows[:].bitcast(F32)[:, first : first + UNIT_TILES, :]
 
-            c_sum = quant.tile([P, TILES, HID], F32)
-            nc.gpsimd.tensor_tensor(
-                out=c_sum[:], in0=c_rows[:, :, 0, :], in1=c_rows[:, :, 1, :], op=ALU.add
+        def combine(unit):
+            if not 0 <= unit < HC_UNITS:
+                return
+            g, part = divmod(unit, GROUP_UNITS)
+            rows = h_rows[g][:, part * UNIT_TILES : (part + 1) * UNIT_TILES, :, :]
+            hc = units.tile([P, UNIT_TILES, K_IN], BF16, name="hc")
+            nc.vector.tensor_tensor(
+                out=hc[:, :, 0:HID], in0=rows[:, :, 0, :], in1=rows[:, :, 1, :], op=ALU.add
+            )
+            nc.vector.tensor_tensor(
+                out=hc[:, :, HID:K_IN], in0=rows[:, :, 0, :], in1=rows[:, :, 1, :], op=ALU.max
+            )
+            unit_pairs[unit] = hc[:].bitcast(F32)
+
+        def turn(unit, gates_idle):
+            if not -W_UNITS <= unit < HC_UNITS:
+                return
+            if gates_idle:
+                turned[unit] = psum_acc.tile([P, PACK // 2, UNIT_ROWS], F32, name="early", tag="acc")
+            else:
+                turned[unit] = psum_rest.tile([P, PACK // 2, UNIT_ROWS], F32, name="turned")
+            for r in range(UNIT_TILES):
+                for v in range(PACK // 2):
+                    nc.tensor.transpose(
+                        turned[unit][:, v, r * P : (r + 1) * P],
+                        unit_pairs[unit][:, r, v * P : (v + 1) * P],
+                        ident_f32[:],
+                    )
+
+        def regroup(unit):
+            if not -W_UNITS <= unit < HC_UNITS:
+                return
+            grouped[unit] = units.tile(
+                [P, UNIT_ROWS, PACK], BF16, name="grouped", align_bytes=64
+            )
+            nc.scalar.copy(
+                out=grouped[unit][:].bitcast(F32), in_=turned[unit][:].rearrange("p v r -> p r v")
             )
 
-            hc = quant.tile([P, TILES, K_IN], BF16)
-            nc.vector.tensor_tensor(
-                out=hc[:, :, 0:HID], in0=h_rows[:, :, 0, :], in1=h_rows[:, :, 1, :], op=ALU.add
-            )
-            nc.vector.tensor_tensor(
-                out=hc[:, :, HID:K_IN], in0=h_rows[:, :, 0, :], in1=h_rows[:, :, 1, :], op=ALU.max
-            )
-            hc_grouped = quant.tile([P, GROUP, PACK], BF16, align_bytes=64)
-            for j in range(0, TILES, 2):
-                k_onto_partitions(
-                    nc, psum_turn, hc[:].bitcast(F32)[:, j : j + 2, :], ident_f32,
-                    hc_grouped[:].bitcast(F32)[:, j * P : (j + 2) * P, :],
-                )
-            hc_codes = quant.tile([P, GROUP], U32, align_bytes=64)
-            hc_scales = quant.tile([P, GROUP], U8, align_bytes=64)
+        def quantise(unit):
+            if not -W_UNITS <= unit < HC_UNITS:
+                return
+            g, part = divmod(unit, GROUP_UNITS)
+            if unit >= 0 and part == 0:
+                hc_codes[g] = codes.tile([P, GROUP], U32, name="hc_codes", align_bytes=64)
+                hc_scales[g] = codes.tile([P, GROUP], U8, name="hc_scales", align_bytes=64)
+            if unit < 0:
+                words, scales, first = w_codes, w_scales, (unit + W_UNITS) * UNIT_ROWS
+            else:
+                words, scales, first = hc_codes[g], hc_scales[g], part * UNIT_ROWS
             nc.vector.quantize_mx(
-                out=hc_codes[:].bitcast(FP8X4),
-                scales=hc_scales[:],
-                in_=hc_grouped[:].rearrange("p n t -> p (n t)"),
+                out=words[:, first : first + UNIT_ROWS].bitcast(FP8X4),
+                scales=scales[:, first : first + UNIT_ROWS],
+                in_=grouped[unit][:].rearrange("p r t -> p (r t)"),
             )
 
-            result = stores.tile([P, TILES, 2 * HID], F32)
-            for half in range(HALVES):
-                feats = slice(half * P, (half + 1) * P)
+        def multiply(step, position):
+            if not 0 <= step < STEPS:
+                return
+            g, half = divmod(step, HALVES)
+            m = GATES[position][0] + half
+            acc[step, position] = psum_acc.tile([P, GROUP], F32, name="acc")
+            nc.tensor.matmul_mx(
+                out=acc[step, position][:],
+                lhsT=w_codes[:, m * P : (m + 1) * P].bitcast(FP8X4),
+                lhsT_scale=w_scales[:, m * P : (m + 1) * P],
+                rhs=hc_codes[g][:].bitcast(FP8X4),
+                rhs_scale=hc_scales[g][:],
+                start=True,
+                stop=True,
+            )
 
-                def gate(first_tile, func, name):
-                    m = first_tile + half
-                    acc = psum_gate.tile([P, GROUP], F32, tag="acc")
-                    nc.tensor.matmul_mx(
-                        out=acc[:],
-                        lhsT=w_codes[:, m * P : (m + 1) * P].bitcast(FP8X4),
-                        lhsT_scale=w_scales[:, m * P : (m + 1) * P],
-                        rhs=hc_codes[:].bitcast(FP8X4),
-                        rhs_scale=hc_scales[:],
-                        start=True,
-                        stop=True,
-                    )
-                    value = gates.tile([P, GROUP], F32, name=name)
-                    nc.scalar.activation(
-                        out=value[:], in_=acc[:], func=func, bias=bias[:, m : m + 1], scale=1.0
-                    )
-                    return value
+        def activate(step, position):
+            if not 0 <= step < STEPS:
+                return
+            first_tile, func = GATES[position]
+            m = first_tile + step % HALVES
+            gate[step, position] = gates.tile([P, GROUP], F32, name="gate%d" % position)
+            nc.scalar.activation(
+                out=gate[step, position][:], in_=acc[step, position][:], func=func,
+                bias=bias[:, m : m + 1], scale=1.0,
+            )
 
-                gate_i = gate(GATE_I, ACT.Sigmoid, "gate_i")
-                gate_u = gate(GATE_U, ACT.Tanh, "gate_u")
-                gate_f = gate(GATE_F, ACT.Sigmoid, "gate_f")
-                gate_o = gate(GATE_O, ACT.Sigmoid, "gate_o")
+        def product(name, in0, in1):
+            value = gates.tile([P, GROUP], F32, name=name)
+            nc.vector.tensor_tensor(out=value[:], in0=in0[:], in1=in1[:], op=ALU.mult)
+            return value
 
-                fresh = gates.tile([P, GROUP], F32)
-                nc.vector.tensor_tensor(out=fresh[:], in0=gate_i[:], in1=gate_u[:], op=ALU.mult)
-
-                def turned_back(value, name):
-                    back = psum_back.tile([P, TILES, P], F32, name=name)
-                    for j in range(TILES):
-                        nc.tensor.transpose(
-                            back[:, j, :], value[:, j * P : (j + 1) * P], ident_f32[:]
-                        )
-                    return back
-
-                gate_f_back = turned_back(gate_f, "gate_f_back")
-                fresh_back = turned_back(fresh, "fresh_back")
-                gate_o_back = turned_back(gate_o, "gate_o_back")
-
-                kept = gates.tile([P, TILES, P], F32)
-                nc.vector.tensor_tensor(
-                    out=kept[:], in0=gate_f_back[:], in1=c_sum[:, :, feats], op=ALU.mult
+        def sum_children(step):
+            if not 0 <= step < STEPS:
+                return
+            g, half = divmod(step, HALVES)
+            c_sum[step] = psum_rest.tile([P, GROUP], F32, name="c_sum")
+            for r in range(PAIR_TILES):
+                nc.tensor.matmul(
+                    out=c_sum[step][:, r * PAIR_NODES : (r + 1) * PAIR_NODES],
+                    lhsT=c_rows[g][:, r, half * P : (half + 1) * P],
+                    rhs=pair_sum[:],
+                    start=True,
+                    stop=True,
                 )
-                c_out = result[:, :, HID + half * P : HID + (half + 1) * P]
-                nc.vector.tensor_tensor(out=c_out, in0=fresh_back[:], in1=kept[:], op=ALU.add)
-                tanh_c = gates.tile([P, TILES, P], F32)
-                nc.scalar.activation(out=tanh_c[:], in_=c_out, func=ACT.Tanh)
-                nc.vector.tensor_tensor(
-                    out=result[:, :, feats], in0=gate_o_back[:], in1=tanh_c[:], op=ALU.mult
+            if half == HALVES - 1:
+                load(g + LOAD_BUFS)
+
+        def turn_back(step):
+            if not 0 <= step < STEPS:
+                return
+            cell_back[step] = psum_rest.tile([P, TILES, P], F32, name="cell_back")
+            o_back[step] = psum_rest.tile([P, TILES, P], F32, name="o_back")
+            for j in range(TILES):
+                nodes = slice(j * P, (j + 1) * P)
+                nc.tensor.matmul(
+                    out=cell_back[step][:, j, :], lhsT=fresh[step][:, nodes], rhs=ident_f32[:],
+                    is_transpose=True, start=True, stop=False,
                 )
-            nc.sync.dma_start(out=out_view[g], in_=result[:])
+                nc.tensor.matmul(
+                    out=cell_back[step][:, j, :], lhsT=kept[step][:, nodes], rhs=ident_f32[:],
+                    is_transpose=True, start=False, stop=True,
+                )
+            for j in range(TILES):
+                nc.tensor.transpose(
+                    o_back[step][:, j, :], gate[step, O][:, j * P : (j + 1) * P], ident_f32[:]
+                )
+
+        def c_columns(step):
+            g, half = divmod(step, HALVES)
+            return result[g][:, :, HID + half * P : HID + (half + 1) * P]
+
+        def h_columns(step):
+            g, half = divmod(step, HALVES)
+            return result[g][:, :, half * P : (half + 1) * P]
+
+        for p in range(FIRST_PERIOD, STEPS + 1):
+            unit = p + LEAD
+            now, last = p, p - 1
+            in_now = 0 <= now < STEPS
+            in_last = 0 <= last < STEPS
+
+            turn_back(last)
+            turn(unit - 1, gates_idle=p < 0)
+            sum_children(now)
+            if in_last:
+                if last % HALVES == 0:
+                    result[last // HALVES] = stores.tile([P, TILES, 2 * HID], F32, name="result")
+                nc.vector.tensor_copy(out=c_columns(last), in_=cell_back[last][:])
+            multiply(now, O)
+
+            activate(now, I)
+            multiply(now + 1, I)
+            activate(now, U)
+            multiply(now + 1, U)
+            if in_now:
+                fresh[now] = product("fresh", gate[now, I], gate[now, U])
+            activate(now, F)
+            multiply(now + 1, F)
+            if in_now:
+                kept[now] = product("kept", gate[now, F], c_sum[now])
+
+            if in_last:
+                tanh_c[last] = gates.tile([P, TILES, P], F32, name="tanh_c")
+                nc.scalar.activation(out=tanh_c[last][:], in_=c_columns(last), func=ACT.Tanh)
+                nc.vector.tensor_tensor(
+                    out=h_columns(last), in0=o_back[last][:], in1=tanh_c[last][:], op=ALU.mult
+                )
+                if last % HALVES == HALVES - 1:
+                    nc.sync.dma_start(out=out_view[last // HALVES], in_=result[last // HALVES][:])
+            activate(now, O)
+
+            combine(unit)
+            regroup(unit - 1)
+            quantise(unit - 2)

@@ -89,12 +89,13 @@ def tile_treelstmcellv2_t_kernel(
             out=bias_rows[F_TILE:W_TILES, :], in_=U_f_b.rearrange("(m c) -> m c", c=P)
         )
         w_rows = const.tile([P, W_TILES, K_IN], BF16)
-        nc.sync.dma_start(
-            out=w_rows[:, 0:F_TILE, :], in_=U_iou_w.rearrange("(m p) k -> p m k", p=P)
-        )
-        nc.sync.dma_start(
-            out=w_rows[:, F_TILE:W_TILES, :], in_=U_f_w.rearrange("(m p) k -> p m k", p=P)
-        )
+        w_tiles_iou = U_iou_w.rearrange("(m p) k -> p m k", p=P)
+        w_tiles_f = U_f_w.rearrange("(m p) k -> p m k", p=P)
+        for m in range(0, F_TILE, UNIT_TILES):
+            nc.sync.dma_start(
+                out=w_rows[:, m : m + UNIT_TILES, :], in_=w_tiles_iou[:, m : m + UNIT_TILES, :]
+            )
+        nc.sync.dma_start(out=w_rows[:, F_TILE:W_TILES, :], in_=w_tiles_f)
         for g in range(LOAD_BUFS):
             load(g)
 
@@ -264,6 +265,11 @@ def tile_treelstmcellv2_t_kernel(
                 if last % HALVES == 0:
                     result[last // HALVES] = stores.tile([P, TILES, 2 * HID], F32, name="result")
                 nc.vector.tensor_copy(out=c_columns(last), in_=cell_back[last][:])
+                if last % HALVES == HALVES - 1:
+                    nc.sync.dma_start(
+                        out=out_view[last // HALVES][:, :, HID : 2 * HID],
+                        in_=result[last // HALVES][:, :, HID : 2 * HID],
+                    )
             multiply(now, O)
 
             activate(now, I)
@@ -284,7 +290,10 @@ def tile_treelstmcellv2_t_kernel(
                     out=h_columns(last), in0=o_back[last][:], in1=tanh_c[last][:], op=ALU.mult
                 )
                 if last % HALVES == HALVES - 1:
-                    nc.sync.dma_start(out=out_view[last // HALVES], in_=result[last // HALVES][:])
+                    nc.sync.dma_start(
+                        out=out_view[last // HALVES][:, :, 0:HID],
+                        in_=result[last // HALVES][:, :, 0:HID],
+                    )
             activate(now, O)
 
             combine(unit)

@@ -42,6 +42,7 @@ GATES = (
 I, U, F, O = 0, 1, 2, 3
 LEAD = 5
 FIRST_PERIOD = 1 - LEAD - W_UNITS
+VECTOR_ROWS = 128
 LOAD_BUFS = 4
 
 FLOPS = 2 * NODES * K_IN * 4 * HID
@@ -99,6 +100,11 @@ def tile_treelstmcellv2_t_kernel(
         for g in range(LOAD_BUFS):
             load(g)
 
+        table_in = const.tile([P, 1], F32)
+        nc.gpsimd.memset(table_in[:], 0.0)
+        table_out = const.tile([P, 1], F32)
+        nc.scalar.activation(out=table_out[:], in_=table_in[:], func=ACT.Sigmoid)
+
         ident_bf = const.tile([P, P], BF16)
         make_identity(nc, ident_bf[:])
         ident_f32 = const.tile([P, P], F32)
@@ -155,9 +161,14 @@ def tile_treelstmcellv2_t_kernel(
             grouped[unit] = units.tile(
                 [P, UNIT_ROWS, PACK], BF16, name="grouped", align_bytes=64
             )
-            nc.scalar.copy(
-                out=grouped[unit][:].bitcast(F32), in_=turned[unit][:].rearrange("p v r -> p r v")
-            )
+            for first, last, copy in (
+                (0, VECTOR_ROWS, nc.vector.tensor_copy),
+                (VECTOR_ROWS, UNIT_ROWS, nc.scalar.copy),
+            ):
+                copy(
+                    out=grouped[unit][:].bitcast(F32)[:, first:last, :],
+                    in_=turned[unit][:, :, first:last].rearrange("p v r -> p r v"),
+                )
 
         def quantise(unit):
             if not -W_UNITS <= unit < HC_UNITS:
@@ -203,9 +214,9 @@ def tile_treelstmcellv2_t_kernel(
                 bias=bias[:, m : m + 1], scale=1.0,
             )
 
-        def product(name, in0, in1):
+        def product(engine, name, in0, in1):
             value = gates.tile([P, GROUP], F32, name=name)
-            nc.vector.tensor_tensor(out=value[:], in0=in0[:], in1=in1[:], op=ALU.mult)
+            engine.tensor_tensor(out=value[:], in0=in0[:], in1=in1[:], op=ALU.mult)
             return value
 
         def sum_children(step):
@@ -277,11 +288,11 @@ def tile_treelstmcellv2_t_kernel(
             activate(now, U)
             multiply(now + 1, U)
             if in_now:
-                fresh[now] = product("fresh", gate[now, I], gate[now, U])
+                fresh[now] = product(nc.gpsimd, "fresh", gate[now, I], gate[now, U])
             activate(now, F)
             multiply(now + 1, F)
             if in_now:
-                kept[now] = product("kept", gate[now, F], c_sum[now])
+                kept[now] = product(nc.vector, "kept", gate[now, F], c_sum[now])
 
             if in_last:
                 tanh_c[last] = gates.tile([P, TILES, P], F32, name="tanh_c")

@@ -42,7 +42,7 @@ GATES = (
 I, U, F, O = 0, 1, 2, 3
 LEAD = 5
 FIRST_PERIOD = 1 - LEAD - W_UNITS
-VECTOR_ROWS = 128
+VECTOR_ROWS = 192
 LOAD_BUFS = 4
 
 FLOPS = 2 * NODES * K_IN * 4 * HID
@@ -155,20 +155,17 @@ def tile_treelstmcellv2_t_kernel(
                         ident_f32[:],
                     )
 
-        def regroup(unit):
-            if not -W_UNITS <= unit < HC_UNITS:
+        def regroup(unit, copy, first, last):
+            if not -W_UNITS <= unit < HC_UNITS or first == last:
                 return
-            grouped[unit] = units.tile(
-                [P, UNIT_ROWS, PACK], BF16, name="grouped", align_bytes=64
-            )
-            for first, last, copy in (
-                (0, VECTOR_ROWS, nc.vector.tensor_copy),
-                (VECTOR_ROWS, UNIT_ROWS, nc.scalar.copy),
-            ):
-                copy(
-                    out=grouped[unit][:].bitcast(F32)[:, first:last, :],
-                    in_=turned[unit][:, :, first:last].rearrange("p v r -> p r v"),
+            if unit not in grouped:
+                grouped[unit] = units.tile(
+                    [P, UNIT_ROWS, PACK], BF16, name="grouped", align_bytes=64
                 )
+            copy(
+                out=grouped[unit][:].bitcast(F32)[:, first:last, :],
+                in_=turned[unit][:, :, first:last].rearrange("p v r -> p r v"),
+            )
 
         def quantise(unit):
             if not -W_UNITS <= unit < HC_UNITS:
@@ -239,7 +236,6 @@ def tile_treelstmcellv2_t_kernel(
             if not 0 <= step < STEPS:
                 return
             cell_back[step] = psum_rest.tile([P, TILES, P], F32, name="cell_back")
-            o_back[step] = psum_rest.tile([P, TILES, P], F32, name="o_back")
             for j in range(TILES):
                 nodes = slice(j * P, (j + 1) * P)
                 nc.tensor.matmul(
@@ -250,6 +246,11 @@ def tile_treelstmcellv2_t_kernel(
                     out=cell_back[step][:, j, :], lhsT=kept[step][:, nodes], rhs=ident_f32[:],
                     is_transpose=True, start=False, stop=True,
                 )
+
+        def turn_o(step):
+            if not 0 <= step < STEPS:
+                return
+            o_back[step] = psum_rest.tile([P, TILES, P], F32, name="o_back")
             for j in range(TILES):
                 nc.tensor.transpose(
                     o_back[step][:, j, :], gate[step, O][:, j * P : (j + 1) * P], ident_f32[:]
@@ -263,50 +264,64 @@ def tile_treelstmcellv2_t_kernel(
             g, half = divmod(step, HALVES)
             return result[g][:, :, half * P : (half + 1) * P]
 
+        def copy_c(step):
+            if not 0 <= step < STEPS:
+                return
+            if step % HALVES == 0:
+                result[step // HALVES] = stores.tile([P, TILES, 2 * HID], F32, name="result")
+            nc.vector.tensor_copy(out=c_columns(step), in_=cell_back[step][:])
+            if step % HALVES == HALVES - 1:
+                nc.sync.dma_start(
+                    out=out_view[step // HALVES][:, :, HID : 2 * HID],
+                    in_=result[step // HALVES][:, :, HID : 2 * HID],
+                )
+
+        def tanh(step):
+            if not 0 <= step < STEPS:
+                return
+            tanh_c[step] = gates.tile([P, TILES, P], F32, name="tanh_c")
+            nc.scalar.activation(out=tanh_c[step][:], in_=cell_back[step][:], func=ACT.Tanh)
+
+        def make_h(step):
+            if not 0 <= step < STEPS:
+                return
+            nc.vector.tensor_tensor(
+                out=h_columns(step), in0=o_back[step][:], in1=tanh_c[step][:], op=ALU.mult
+            )
+            if step % HALVES == HALVES - 1:
+                nc.sync.dma_start(
+                    out=out_view[step // HALVES][:, :, 0:HID],
+                    in_=result[step // HALVES][:, :, 0:HID],
+                )
+
+        def make_fresh(step):
+            if 0 <= step < STEPS:
+                fresh[step] = product(nc.gpsimd, "fresh", gate[step, I], gate[step, U])
+
+        def make_kept(step):
+            if 0 <= step < STEPS:
+                kept[step] = product(nc.vector, "kept", gate[step, F], c_sum[step])
+
         for p in range(FIRST_PERIOD, STEPS + 1):
             unit = p + LEAD
-            now, last = p, p - 1
-            in_now = 0 <= now < STEPS
-            in_last = 0 <= last < STEPS
-
-            turn_back(last)
+            turn_back(p - 1)
+            turn_o(p - 1)
             turn(unit - 1, gates_idle=p < 0)
-            sum_children(now)
-            if in_last:
-                if last % HALVES == 0:
-                    result[last // HALVES] = stores.tile([P, TILES, 2 * HID], F32, name="result")
-                nc.vector.tensor_copy(out=c_columns(last), in_=cell_back[last][:])
-                if last % HALVES == HALVES - 1:
-                    nc.sync.dma_start(
-                        out=out_view[last // HALVES][:, :, HID : 2 * HID],
-                        in_=result[last // HALVES][:, :, HID : 2 * HID],
-                    )
-            multiply(now, O)
-
-            activate(now, I)
-            multiply(now + 1, I)
-            activate(now, U)
-            multiply(now + 1, U)
-            if in_now:
-                fresh[now] = product(nc.gpsimd, "fresh", gate[now, I], gate[now, U])
-            activate(now, F)
-            multiply(now + 1, F)
-            if in_now:
-                kept[now] = product(nc.vector, "kept", gate[now, F], c_sum[now])
-
-            if in_last:
-                tanh_c[last] = gates.tile([P, TILES, P], F32, name="tanh_c")
-                nc.scalar.activation(out=tanh_c[last][:], in_=c_columns(last), func=ACT.Tanh)
-                nc.vector.tensor_tensor(
-                    out=h_columns(last), in0=o_back[last][:], in1=tanh_c[last][:], op=ALU.mult
-                )
-                if last % HALVES == HALVES - 1:
-                    nc.sync.dma_start(
-                        out=out_view[last // HALVES][:, :, 0:HID],
-                        in_=result[last // HALVES][:, :, 0:HID],
-                    )
-            activate(now, O)
-
+            multiply(p, O)
+            activate(p, F)
+            multiply(p + 1, F)
+            make_kept(p)
             combine(unit)
-            regroup(unit - 1)
+            activate(p, I)
+            multiply(p + 1, I)
+            activate(p, U)
+            multiply(p + 1, U)
+            sum_children(p + 1)
+            make_fresh(p)
+            regroup(unit - 1, nc.vector.tensor_copy, 0, VECTOR_ROWS)
+            tanh(p - 1)
+            copy_c(p - 1)
+            activate(p, O)
+            make_h(p - 1)
+            regroup(unit - 1, nc.scalar.copy, VECTOR_ROWS, UNIT_ROWS)
             quantise(unit - 2)

@@ -42,7 +42,7 @@ GATES = (
 I, U, F, O = 0, 1, 2, 3
 LEAD = 5
 FIRST_PERIOD = 1 - LEAD - W_UNITS
-VECTOR_ROWS = 192
+VECTOR_ROWS = 176
 LOAD_BUFS = 4
 
 FLOPS = 2 * NODES * K_IN * 4 * HID
@@ -304,14 +304,14 @@ def tile_treelstmcellv2_t_kernel(
 
         for p in range(FIRST_PERIOD, STEPS + 1):
             unit = p + LEAD
+            turn(unit - 1, gates_idle=p < 0)
             turn_back(p - 1)
             turn_o(p - 1)
-            turn(unit - 1, gates_idle=p < 0)
             multiply(p, O)
             activate(p, F)
             multiply(p + 1, F)
-            make_kept(p)
             combine(unit)
+            make_kept(p)
             activate(p, I)
             multiply(p + 1, I)
             activate(p, U)

@@ -24,6 +24,7 @@ HALVES = HID // P
 STEPS = N_GROUPS * HALVES
 PAIR_NODES = P // CHILDREN
 PAIR_TILES = GROUP // PAIR_NODES
+PAIR_PLACES = PAIR_NODES // TILES
 
 UNIT_TILES = 2
 UNIT_ROWS = UNIT_TILES * P
@@ -52,8 +53,8 @@ def tile_treelstmcellv2_t_kernel(
     tc, mailbox_h, mailbox_c, U_iou_w, b_iou, U_f_w, U_f_b, out
 ):
     nc = tc.nc
-    h_view = mailbox_h.rearrange("(g j p) k f -> g p j k f", j=TILES, p=P)
-    out_view = out.rearrange("(g j p) c -> g p j c", j=TILES, p=P)
+    h_view = mailbox_h.rearrange("(g p j) k f -> g p j k f", j=TILES, p=P)
+    out_view = out.rearrange("(g p j) c -> g p j c", j=TILES, p=P)
     c_view = mailbox_c.rearrange("n k f -> (n k) f").rearrange(
         "(g r p) f -> g p r f", r=PAIR_TILES, p=P
     )
@@ -109,10 +110,12 @@ def tile_treelstmcellv2_t_kernel(
         make_identity(nc, ident_bf[:])
         ident_f32 = const.tile([P, P], F32)
         make_identity(nc, ident_f32[:])
-        pair_sum = const.tile([P, PAIR_NODES], BF16)
-        ident_pairs = ident_bf[:].rearrange("p (n two) -> p two n", two=CHILDREN)
+        pair_sum = const.tile([P, TILES, PAIR_PLACES], BF16)
+        ident_pairs = ident_bf[:].rearrange(
+            "p (s j two) -> p two j s", j=TILES, two=CHILDREN
+        )
         nc.vector.tensor_tensor(
-            out=pair_sum[:], in0=ident_pairs[:, 0, :], in1=ident_pairs[:, 1, :], op=ALU.add
+            out=pair_sum[:], in0=ident_pairs[:, 0], in1=ident_pairs[:, 1], op=ALU.add
         )
 
         bias_turned = psum_rest.tile([P, P], BF16, tag="turned")
@@ -213,17 +216,17 @@ def tile_treelstmcellv2_t_kernel(
 
         def product(engine, name, in0, in1):
             value = gates.tile([P, GROUP], F32, name=name)
-            engine.tensor_tensor(out=value[:], in0=in0[:], in1=in1[:], op=ALU.mult)
+            engine.tensor_tensor(out=value[:], in0=in0, in1=in1, op=ALU.mult)
             return value
 
         def sum_children(step):
             if not 0 <= step < STEPS:
                 return
             g, half = divmod(step, HALVES)
-            c_sum[step] = psum_rest.tile([P, GROUP], F32, name="c_sum")
+            c_sum[step] = psum_rest.tile([P, TILES, P], F32, name="c_sum")
             for r in range(PAIR_TILES):
                 nc.tensor.matmul(
-                    out=c_sum[step][:, r * PAIR_NODES : (r + 1) * PAIR_NODES],
+                    out=c_sum[step][:, :, r * PAIR_PLACES : (r + 1) * PAIR_PLACES],
                     lhsT=c_rows[g][:, r, half * P : (half + 1) * P],
                     rhs=pair_sum[:],
                     start=True,
@@ -270,7 +273,7 @@ def tile_treelstmcellv2_t_kernel(
             if step % HALVES == 0:
                 result[step // HALVES] = stores.tile([P, TILES, 2 * HID], F32, name="result")
             nc.vector.tensor_copy(out=c_columns(step), in_=cell_back[step][:])
-            if step % HALVES == HALVES - 1:
+            if step == STEPS - 1:
                 nc.sync.dma_start(
                     out=out_view[step // HALVES][:, :, HID : 2 * HID],
                     in_=result[step // HALVES][:, :, HID : 2 * HID],
@@ -289,18 +292,19 @@ def tile_treelstmcellv2_t_kernel(
                 out=h_columns(step), in0=o_back[step][:], in1=tanh_c[step][:], op=ALU.mult
             )
             if step % HALVES == HALVES - 1:
+                columns = slice(0, HID if step == STEPS - 1 else 2 * HID)
                 nc.sync.dma_start(
-                    out=out_view[step // HALVES][:, :, 0:HID],
-                    in_=result[step // HALVES][:, :, 0:HID],
+                    out=out_view[step // HALVES][:, :, columns],
+                    in_=result[step // HALVES][:, :, columns],
                 )
 
         def make_fresh(step):
             if 0 <= step < STEPS:
-                fresh[step] = product(nc.gpsimd, "fresh", gate[step, I], gate[step, U])
+                fresh[step] = product(nc.gpsimd, "fresh", gate[step, I][:], gate[step, U][:])
 
         def make_kept(step):
             if 0 <= step < STEPS:
-                kept[step] = product(nc.vector, "kept", gate[step, F], c_sum[step])
+                kept[step] = product(nc.vector, "kept", gate[step, F][:], c_sum[step][:].rearrange("p j n -> p (j n)"))
 
         for p in range(FIRST_PERIOD, STEPS + 1):
             unit = p + LEAD

@@ -26,6 +26,7 @@ PAIR_NODES = P // CHILDREN
 PAIR_TILES = GROUP // PAIR_NODES
 PAIR_PLACES = PAIR_NODES // TILES
 
+ALL_TILES = slice(0, TILES)
 UNIT_TILES = 2
 UNIT_ROWS = UNIT_TILES * P
 GROUP_UNITS = GROUP // UNIT_ROWS
@@ -42,8 +43,8 @@ GATES = (
 )
 I, U, F, O = 0, 1, 2, 3
 LEAD = 5
-FIRST_PERIOD = 1 - LEAD - W_UNITS
 VECTOR_ROWS = 176
+HEAD_VECTOR_ROWS = 64
 LOAD_BUFS = 4
 
 FLOPS = 2 * NODES * K_IN * 4 * HID
@@ -62,44 +63,57 @@ def tile_treelstmcellv2_t_kernel(
     with ExitStack() as ctx:
         const = ctx.enter_context(tc.tile_pool(name="const", bufs=1))
         loads = ctx.enter_context(tc.tile_pool(name="loads", bufs=LOAD_BUFS))
-        units = ctx.enter_context(tc.tile_pool(name="units", bufs=3))
+        units = ctx.enter_context(tc.tile_pool(name="units", bufs=4))
         codes = ctx.enter_context(tc.tile_pool(name="codes", bufs=4))
         gates = ctx.enter_context(tc.tile_pool(name="gates", bufs=2))
         stores = ctx.enter_context(tc.tile_pool(name="stores", bufs=3))
-        psum_acc = ctx.enter_context(tc.psum_pool(name="psum_acc", bufs=len(GATES)))
-        psum_rest = ctx.enter_context(tc.psum_pool(name="psum_rest", bufs=1))
+        psum = ctx.enter_context(tc.psum_pool(name="psum", bufs=1))
         ctx.enter_context(tc.manual_schedule())
 
         h_rows, c_rows, unit_pairs, turned, grouped = {}, {}, {}, {}, {}
         hc_codes, hc_scales, acc, gate, c_sum = {}, {}, {}, {}, {}
         fresh, kept, cell_back, o_back, tanh_c, result = {}, {}, {}, {}, {}, {}
 
-        def load(g):
-            if g >= N_GROUPS:
-                return
+        def load_h(g, pieces):
             h_rows[g] = loads.tile([P, TILES, CHILDREN, HID], BF16, name="h_rows")
-            nc.sync.dma_start(out=h_rows[g][:], in_=h_view[g])
+            width = TILES // pieces
+            for first in range(0, TILES, width):
+                tiles = slice(first, first + width)
+                nc.sync.dma_start(out=h_rows[g][:, tiles], in_=h_view[g][:, tiles])
+
+        def load_c(g):
             c_rows[g] = loads.tile([P, PAIR_TILES, HID], BF16, name="c_rows")
             nc.sync.dma_start(out=c_rows[g][:], in_=c_view[g])
 
+        def load(g):
+            if g < N_GROUPS:
+                load_h(g, 1)
+                load_c(g)
+
         bias_rows = const.tile([P, P], BF16)
         nc.vector.memset(bias_rows[:], 0.0)
+        w_rows = const.tile([P, W_TILES, K_IN], BF16)
+        w_tiles_iou = U_iou_w.rearrange("(m p) k -> p m k", p=P)
+        w_tiles_f = U_f_w.rearrange("(m p) k -> p m k", p=P)
+        nc.sync.dma_start(out=w_rows[:, F_TILE:W_TILES, :], in_=w_tiles_f)
+        load_h(0, GROUP_UNITS)
         nc.sync.dma_start(
             out=bias_rows[0:F_TILE, :], in_=b_iou.rearrange("o (m c) -> (o m) c", c=P)
         )
         nc.sync.dma_start(
             out=bias_rows[F_TILE:W_TILES, :], in_=U_f_b.rearrange("(m c) -> m c", c=P)
         )
-        w_rows = const.tile([P, W_TILES, K_IN], BF16)
-        w_tiles_iou = U_iou_w.rearrange("(m p) k -> p m k", p=P)
-        w_tiles_f = U_f_w.rearrange("(m p) k -> p m k", p=P)
-        for m in range(0, F_TILE, UNIT_TILES):
+        for position in (I, U, O):
+            m = GATES[position][0]
             nc.sync.dma_start(
                 out=w_rows[:, m : m + UNIT_TILES, :], in_=w_tiles_iou[:, m : m + UNIT_TILES, :]
             )
-        nc.sync.dma_start(out=w_rows[:, F_TILE:W_TILES, :], in_=w_tiles_f)
-        for g in range(LOAD_BUFS):
-            load(g)
+        load_h(1, GROUP_UNITS)
+        load_c(0)
+        for g in range(2, LOAD_BUFS):
+            load_h(g, 1)
+            load_c(g - 1)
+        load_c(LOAD_BUFS - 1)
 
         table_in = const.tile([P, 1], F32)
         nc.gpsimd.memset(table_in[:], 0.0)
@@ -117,11 +131,6 @@ def tile_treelstmcellv2_t_kernel(
         nc.vector.tensor_tensor(
             out=pair_sum[:], in0=ident_pairs[:, 0], in1=ident_pairs[:, 1], op=ALU.add
         )
-
-        bias_turned = psum_rest.tile([P, P], BF16, tag="turned")
-        nc.tensor.transpose(bias_turned[:], bias_rows[:], ident_bf[:])
-        bias = const.tile([P, W_TILES], F32)
-        nc.vector.tensor_copy(out=bias[:], in_=bias_turned[:, 0:W_TILES])
 
         w_codes = const.tile([P, W_TILES * P], U32, align_bytes=64)
         w_scales = const.tile([P, W_TILES * P], U8, align_bytes=64)
@@ -143,13 +152,10 @@ def tile_treelstmcellv2_t_kernel(
             )
             unit_pairs[unit] = hc[:].bitcast(F32)
 
-        def turn(unit, gates_idle):
+        def turn(unit, bank):
             if not -W_UNITS <= unit < HC_UNITS:
                 return
-            if gates_idle:
-                turned[unit] = psum_acc.tile([P, PACK // 2, UNIT_ROWS], F32, name="early", tag="acc")
-            else:
-                turned[unit] = psum_rest.tile([P, PACK // 2, UNIT_ROWS], F32, name="turned")
+            turned[unit] = psum.tile([P, PACK // 2, UNIT_ROWS], F32, name="turned", tag=bank)
             for r in range(UNIT_TILES):
                 for v in range(PACK // 2):
                     nc.tensor.transpose(
@@ -192,7 +198,7 @@ def tile_treelstmcellv2_t_kernel(
                 return
             g, half = divmod(step, HALVES)
             m = GATES[position][0] + half
-            acc[step, position] = psum_acc.tile([P, GROUP], F32, name="acc")
+            acc[step, position] = psum.tile([P, GROUP], F32, name="acc", tag="acc%d" % position)
             nc.tensor.matmul_mx(
                 out=acc[step, position][:],
                 lhsT=w_codes[:, m * P : (m + 1) * P].bitcast(FP8X4),
@@ -223,7 +229,7 @@ def tile_treelstmcellv2_t_kernel(
             if not 0 <= step < STEPS:
                 return
             g, half = divmod(step, HALVES)
-            c_sum[step] = psum_rest.tile([P, TILES, P], F32, name="c_sum")
+            c_sum[step] = psum.tile([P, TILES, P], F32, name="c_sum")
             for r in range(PAIR_TILES):
                 nc.tensor.matmul(
                     out=c_sum[step][:, :, r * PAIR_PLACES : (r + 1) * PAIR_PLACES],
@@ -235,10 +241,8 @@ def tile_treelstmcellv2_t_kernel(
             if half == HALVES - 1:
                 load(g + LOAD_BUFS)
 
-        def turn_back(step):
-            if not 0 <= step < STEPS:
-                return
-            cell_back[step] = psum_rest.tile([P, TILES, P], F32, name="cell_back")
+        def turn_back(step, bank="cell_back"):
+            cell_back[step] = psum.tile([P, TILES, P], F32, name="cell_back", tag=bank)
             for j in range(TILES):
                 nodes = slice(j * P, (j + 1) * P)
                 nc.tensor.matmul(
@@ -250,10 +254,8 @@ def tile_treelstmcellv2_t_kernel(
                     is_transpose=True, start=False, stop=True,
                 )
 
-        def turn_o(step):
-            if not 0 <= step < STEPS:
-                return
-            o_back[step] = psum_rest.tile([P, TILES, P], F32, name="o_back")
+        def turn_o(step, bank="o_back"):
+            o_back[step] = psum.tile([P, TILES, P], F32, name="o_back", tag=bank)
             for j in range(TILES):
                 nc.tensor.transpose(
                     o_back[step][:, j, :], gate[step, O][:, j * P : (j + 1) * P], ident_f32[:]
@@ -267,53 +269,114 @@ def tile_treelstmcellv2_t_kernel(
             g, half = divmod(step, HALVES)
             return result[g][:, :, half * P : (half + 1) * P]
 
-        def copy_c(step):
-            if not 0 <= step < STEPS:
+        def store(step, first, tiles):
+            g, half = divmod(step, HALVES)
+            if g == N_GROUPS - 1:
+                columns = slice(first + half * P, first + (half + 1) * P)
+            elif half == HALVES - 1 and first == 0:
+                columns = slice(0, 2 * HID)
+            else:
                 return
+            nc.sync.dma_start(
+                out=out_view[g][:, tiles, columns], in_=result[g][:, tiles, columns]
+            )
+
+        def copy_c(step, tiles=ALL_TILES):
             if step % HALVES == 0:
                 result[step // HALVES] = stores.tile([P, TILES, 2 * HID], F32, name="result")
-            nc.vector.tensor_copy(out=c_columns(step), in_=cell_back[step][:])
-            if step == STEPS - 1:
-                nc.sync.dma_start(
-                    out=out_view[step // HALVES][:, :, HID : 2 * HID],
-                    in_=result[step // HALVES][:, :, HID : 2 * HID],
-                )
-
-        def tanh(step):
-            if not 0 <= step < STEPS:
-                return
-            tanh_c[step] = gates.tile([P, TILES, P], F32, name="tanh_c")
-            nc.scalar.activation(out=tanh_c[step][:], in_=cell_back[step][:], func=ACT.Tanh)
-
-        def make_h(step):
-            if not 0 <= step < STEPS:
-                return
-            nc.vector.tensor_tensor(
-                out=h_columns(step), in0=o_back[step][:], in1=tanh_c[step][:], op=ALU.mult
+            nc.vector.tensor_copy(
+                out=c_columns(step)[:, tiles], in_=cell_back[step][:, tiles]
             )
-            if step % HALVES == HALVES - 1:
-                columns = slice(0, HID if step == STEPS - 1 else 2 * HID)
-                nc.sync.dma_start(
-                    out=out_view[step // HALVES][:, :, columns],
-                    in_=result[step // HALVES][:, :, columns],
-                )
+            store(step, HID, tiles)
+
+        def tanh(step, tiles=ALL_TILES):
+            if step not in tanh_c:
+                tanh_c[step] = gates.tile([P, TILES, P], F32, name="tanh_c")
+            nc.scalar.activation(
+                out=tanh_c[step][:, tiles], in_=cell_back[step][:, tiles], func=ACT.Tanh
+            )
+
+        def make_h(step, tiles=ALL_TILES):
+            nc.vector.tensor_tensor(
+                out=h_columns(step)[:, tiles], in0=tanh_c[step][:, tiles],
+                in1=o_back[step][:, tiles], op=ALU.mult,
+            )
+            store(step, 0, tiles)
 
         def make_fresh(step):
             if 0 <= step < STEPS:
-                fresh[step] = product(nc.gpsimd, "fresh", gate[step, I][:], gate[step, U][:])
+                engine = nc.vector if step == STEPS - 1 else nc.gpsimd
+                fresh[step] = product(engine, "fresh", gate[step, I][:], gate[step, U][:])
 
         def make_kept(step):
             if 0 <= step < STEPS:
                 kept[step] = product(nc.vector, "kept", gate[step, F][:], c_sum[step][:].rearrange("p j n -> p (j n)"))
 
-        for p in range(FIRST_PERIOD, STEPS + 1):
+        def regroup_shared(unit, rows):
+            regroup(unit, nc.scalar.copy, rows, UNIT_ROWS)
+            regroup(unit, nc.vector.tensor_copy, 0, rows)
+
+        w_unit = {position: GATES[position][0] // UNIT_TILES - W_UNITS for position in (I, U, F, O)}
+        turn(w_unit[F], "acc%d" % O)
+        regroup(w_unit[F], nc.scalar.copy, 0, UNIT_ROWS)
+        combine(0)
+        turn(0, "acc%d" % U)
+        regroup(0, nc.scalar.copy, 0, UNIT_ROWS)
+        combine(1)
+        quantise(w_unit[F])
+        turn(1, "acc%d" % I)
+        regroup(1, nc.scalar.copy, 0, UNIT_ROWS)
+        quantise(0)
+        turn(w_unit[I], "turned")
+        regroup(w_unit[I], nc.scalar.copy, 0, UNIT_ROWS)
+        bias_turned = psum.tile([P, P], BF16, tag="c_sum")
+        nc.tensor.transpose(bias_turned[:], bias_rows[:], ident_bf[:])
+        bias = const.tile([P, W_TILES], F32)
+        nc.vector.tensor_copy(out=bias[:], in_=bias_turned[:, 0:W_TILES])
+        turn(w_unit[U], "cell_back")
+        quantise(1)
+        multiply(0, F)
+        turn(w_unit[O], "o_back")
+        quantise(w_unit[I])
+        multiply(0, I)
+        activate(0, F)
+        regroup(w_unit[U], nc.vector.tensor_copy, 0, UNIT_ROWS)
+        combine(2)
+        activate(0, I)
+        quantise(w_unit[U])
+        turn(2, "turned")
+        multiply(0, U)
+        multiply(1, F)
+        regroup(w_unit[O], nc.vector.tensor_copy, 0, UNIT_ROWS)
+        combine(3)
+        activate(0, U)
+        sum_children(0)
+        quantise(w_unit[O])
+        turn(3, "cell_back")
+        multiply(0, O)
+        multiply(1, I)
+        make_kept(0)
+        make_fresh(0)
+        regroup(2, nc.vector.tensor_copy, 0, UNIT_ROWS)
+        activate(0, O)
+        sum_children(1)
+        combine(4)
+        quantise(2)
+        turn(4, "turned")
+        regroup(3, nc.scalar.copy, 0, UNIT_ROWS)
+        multiply(1, U)
+        combine(5)
+        quantise(3)
+        regroup(4, nc.vector.tensor_copy, 0, UNIT_ROWS)
+
+        for p in range(1, STEPS):
             unit = p + LEAD
-            turn(unit - 1, gates_idle=p < 0)
+            turn(unit - 1, "turned")
             turn_back(p - 1)
-            turn_o(p - 1)
             multiply(p, O)
             activate(p, F)
             multiply(p + 1, F)
+            turn_o(p - 1)
             combine(unit)
             make_kept(p)
             activate(p, I)
@@ -329,3 +392,12 @@ def tile_treelstmcellv2_t_kernel(
             make_h(p - 1)
             regroup(unit - 1, nc.scalar.copy, VECTOR_ROWS, UNIT_ROWS)
             quantise(unit - 2)
+
+        last = STEPS - 1
+        turn_back(last, "acc%d" % I)
+        turn_o(last, "acc%d" % U)
+        for first in range(0, TILES, TILES // 2):
+            tiles = slice(first, first + TILES // 2)
+            tanh(last, tiles)
+            copy_c(last, tiles)
+            make_h(last, tiles)

@@ -43,7 +43,7 @@ GATES = (
 )
 I, U, F, O = 0, 1, 2, 3
 LEAD = 5
-VECTOR_ROWS = 176
+VECTOR_ROWS = 112
 HEAD_VECTOR_ROWS = 64
 LOAD_BUFS = 4
 

@@ -42,9 +42,8 @@ GATES = (
     (1 * HALVES, ACT.Sigmoid),
 )
 I, U, F, O = 0, 1, 2, 3
-LEAD = 5
-VECTOR_ROWS = 112
-HEAD_VECTOR_ROWS = 64
+LEAD = 4
+VECTOR_ROWS = 128
 LOAD_BUFS = 4
 
 FLOPS = 2 * NODES * K_IN * 4 * HID
@@ -312,10 +311,6 @@ def tile_treelstmcellv2_t_kernel(
             if 0 <= step < STEPS:
                 kept[step] = product(nc.vector, "kept", gate[step, F][:], c_sum[step][:].rearrange("p j n -> p (j n)"))
 
-        def regroup_shared(unit, rows):
-            regroup(unit, nc.scalar.copy, rows, UNIT_ROWS)
-            regroup(unit, nc.vector.tensor_copy, 0, rows)
-
         w_unit = {position: GATES[position][0] // UNIT_TILES - W_UNITS for position in (I, U, F, O)}
         turn(w_unit[F], "acc%d" % O)
         regroup(w_unit[F], nc.scalar.copy, 0, UNIT_ROWS)
@@ -339,35 +334,32 @@ def tile_treelstmcellv2_t_kernel(
         turn(w_unit[O], "o_back")
         quantise(w_unit[I])
         multiply(0, I)
-        activate(0, F)
-        regroup(w_unit[U], nc.vector.tensor_copy, 0, UNIT_ROWS)
+        regroup(w_unit[U], nc.scalar.copy, 0, UNIT_ROWS)
         combine(2)
-        activate(0, I)
-        quantise(w_unit[U])
+        activate(0, F)
         turn(2, "turned")
+        quantise(w_unit[U])
         multiply(0, U)
-        multiply(1, F)
         regroup(w_unit[O], nc.vector.tensor_copy, 0, UNIT_ROWS)
+        activate(0, I)
+        multiply(1, F)
         combine(3)
-        activate(0, U)
         sum_children(0)
-        quantise(w_unit[O])
+        activate(0, U)
         turn(3, "cell_back")
+        quantise(w_unit[O])
         multiply(0, O)
         multiply(1, I)
+        regroup(2, nc.scalar.copy, 0, UNIT_ROWS)
         make_kept(0)
         make_fresh(0)
-        regroup(2, nc.vector.tensor_copy, 0, UNIT_ROWS)
+        regroup(3, nc.vector.tensor_copy, 0, UNIT_ROWS)
         activate(0, O)
         sum_children(1)
-        combine(4)
         quantise(2)
-        turn(4, "turned")
-        regroup(3, nc.scalar.copy, 0, UNIT_ROWS)
         multiply(1, U)
-        combine(5)
+        combine(4)
         quantise(3)
-        regroup(4, nc.vector.tensor_copy, 0, UNIT_ROWS)
 
         for p in range(1, STEPS):
             unit = p + LEAD
@@ -391,7 +383,7 @@ def tile_treelstmcellv2_t_kernel(
             activate(p, O)
             make_h(p - 1)
             regroup(unit - 1, nc.scalar.copy, VECTOR_ROWS, UNIT_ROWS)
-            quantise(unit - 2)
+            quantise(unit - 1)
 
         last = STEPS - 1
         turn_back(last, "acc%d" % I)

@@ -43,7 +43,7 @@ GATES = (
 )
 I, U, F, O = 0, 1, 2, 3
 LEAD = 4
-VECTOR_ROWS = 128
+VECTOR_ROWS = 160
 LOAD_BUFS = 4
 
 FLOPS = 2 * NODES * K_IN * 4 * HID
@@ -358,29 +358,30 @@ def tile_treelstmcellv2_t_kernel(
         sum_children(1)
         quantise(2)
         multiply(1, U)
+        multiply(1, O)
         combine(4)
         quantise(3)
 
         for p in range(1, STEPS):
             unit = p + LEAD
-            turn(unit - 1, "turned")
             turn_back(p - 1)
-            multiply(p, O)
+            turn(unit - 1, "turned")
+            turn_o(p - 1)
             activate(p, F)
             multiply(p + 1, F)
-            turn_o(p - 1)
             combine(unit)
             make_kept(p)
             activate(p, I)
             multiply(p + 1, I)
             activate(p, U)
             multiply(p + 1, U)
-            sum_children(p + 1)
             make_fresh(p)
             regroup(unit - 1, nc.vector.tensor_copy, 0, VECTOR_ROWS)
             tanh(p - 1)
             copy_c(p - 1)
             activate(p, O)
+            multiply(p + 1, O)
+            sum_children(p + 1)
             make_h(p - 1)
             regroup(unit - 1, nc.scalar.copy, VECTOR_ROWS, UNIT_ROWS)
             quantise(unit - 1)

@@ -27,6 +27,7 @@ PAIR_TILES = GROUP // PAIR_NODES
 PAIR_PLACES = PAIR_NODES // TILES
 
 ALL_TILES = slice(0, TILES)
+PAIRED_TILES = 3
 UNIT_TILES = 2
 UNIT_ROWS = UNIT_TILES * P
 GROUP_UNITS = GROUP // UNIT_ROWS
@@ -43,7 +44,7 @@ GATES = (
 )
 I, U, F, O = 0, 1, 2, 3
 LEAD = 4
-VECTOR_ROWS = 160
+VECTOR_ROWS = 144
 LOAD_BUFS = 4
 
 FLOPS = 2 * NODES * K_IN * 4 * HID
@@ -71,6 +72,7 @@ def tile_treelstmcellv2_t_kernel(
 
         h_rows, c_rows, unit_pairs, turned, grouped = {}, {}, {}, {}, {}
         hc_codes, hc_scales, acc, gate, c_sum = {}, {}, {}, {}, {}
+        added = {}
         fresh, kept, cell_back, o_back, tanh_c, result = {}, {}, {}, {}, {}, {}
 
         def load_h(g, pieces):
@@ -242,7 +244,7 @@ def tile_treelstmcellv2_t_kernel(
 
         def turn_back(step, bank="cell_back"):
             cell_back[step] = psum.tile([P, TILES, P], F32, name="cell_back", tag=bank)
-            for j in range(TILES):
+            for j in range(PAIRED_TILES if step < STEPS - 1 else TILES):
                 nodes = slice(j * P, (j + 1) * P)
                 nc.tensor.matmul(
                     out=cell_back[step][:, j, :], lhsT=fresh[step][:, nodes], rhs=ident_f32[:],
@@ -251,6 +253,22 @@ def tile_treelstmcellv2_t_kernel(
                 nc.tensor.matmul(
                     out=cell_back[step][:, j, :], lhsT=kept[step][:, nodes], rhs=ident_f32[:],
                     is_transpose=True, start=False, stop=True,
+                )
+
+        def add_terms(step):
+            if step == STEPS - 1:
+                return
+            added[step] = gates.tile([P, (TILES - PAIRED_TILES) * P], F32, name="added")
+            nodes = slice(PAIRED_TILES * P, GROUP)
+            nc.vector.tensor_tensor(
+                out=added[step][:], in0=fresh[step][:, nodes], in1=kept[step][:, nodes], op=ALU.add
+            )
+
+        def turn_sum_back(step):
+            for j in range(PAIRED_TILES, TILES):
+                nodes = slice((j - PAIRED_TILES) * P, (j - PAIRED_TILES + 1) * P)
+                nc.tensor.transpose(
+                    cell_back[step][:, j, :], added[step][:, nodes], ident_f32[:]
                 )
 
         def turn_o(step, bank="o_back"):
@@ -353,6 +371,7 @@ def tile_treelstmcellv2_t_kernel(
         regroup(2, nc.scalar.copy, 0, UNIT_ROWS)
         make_kept(0)
         make_fresh(0)
+        add_terms(0)
         regroup(3, nc.vector.tensor_copy, 0, UNIT_ROWS)
         activate(0, O)
         sum_children(1)
@@ -365,6 +384,7 @@ def tile_treelstmcellv2_t_kernel(
         for p in range(1, STEPS):
             unit = p + LEAD
             turn_back(p - 1)
+            turn_sum_back(p - 1)
             turn(unit - 1, "turned")
             turn_o(p - 1)
             activate(p, F)
@@ -383,6 +403,7 @@ def tile_treelstmcellv2_t_kernel(
             multiply(p + 1, O)
             sum_children(p + 1)
             make_h(p - 1)
+            add_terms(p)
             regroup(unit - 1, nc.scalar.copy, VECTOR_ROWS, UNIT_ROWS)
             quantise(unit - 1)
 

@@ -242,18 +242,27 @@ def tile_treelstmcellv2_t_kernel(
             if half == HALVES - 1:
                 load(g + LOAD_BUFS)
 
-        def turn_back(step, bank="cell_back"):
-            cell_back[step] = psum.tile([P, TILES, P], F32, name="cell_back", tag=bank)
-            for j in range(PAIRED_TILES if step < STEPS - 1 else TILES):
+        def turn_terms(step, bank, first, last):
+            for j in range(first, last):
                 nodes = slice(j * P, (j + 1) * P)
                 nc.tensor.matmul(
-                    out=cell_back[step][:, j, :], lhsT=fresh[step][:, nodes], rhs=ident_f32[:],
+                    out=bank[:, j - first, :], lhsT=fresh[step][:, nodes], rhs=ident_f32[:],
                     is_transpose=True, start=True, stop=False,
                 )
                 nc.tensor.matmul(
-                    out=cell_back[step][:, j, :], lhsT=kept[step][:, nodes], rhs=ident_f32[:],
+                    out=bank[:, j - first, :], lhsT=kept[step][:, nodes], rhs=ident_f32[:],
                     is_transpose=True, start=False, stop=True,
                 )
+
+        def turn_gate_o(step, bank, first, last):
+            for j in range(first, last):
+                nc.tensor.transpose(
+                    bank[:, j - first, :], gate[step, O][:, j * P : (j + 1) * P], ident_f32[:]
+                )
+
+        def turn_back(step):
+            cell_back[step] = psum.tile([P, TILES, P], F32, name="cell_back")
+            turn_terms(step, cell_back[step], 0, PAIRED_TILES)
 
         def add_terms(step):
             if step == STEPS - 1:
@@ -271,12 +280,9 @@ def tile_treelstmcellv2_t_kernel(
                     cell_back[step][:, j, :], added[step][:, nodes], ident_f32[:]
                 )
 
-        def turn_o(step, bank="o_back"):
-            o_back[step] = psum.tile([P, TILES, P], F32, name="o_back", tag=bank)
-            for j in range(TILES):
-                nc.tensor.transpose(
-                    o_back[step][:, j, :], gate[step, O][:, j * P : (j + 1) * P], ident_f32[:]
-                )
+        def turn_o(step):
+            o_back[step] = psum.tile([P, TILES, P], F32, name="o_back")
+            turn_gate_o(step, o_back[step], 0, TILES)
 
         def c_columns(step):
             g, half = divmod(step, HALVES)
@@ -288,7 +294,7 @@ def tile_treelstmcellv2_t_kernel(
 
         def store(step, first, tiles):
             g, half = divmod(step, HALVES)
-            if g == N_GROUPS - 1:
+            if g >= N_GROUPS - 2:
                 columns = slice(first + half * P, first + (half + 1) * P)
             elif half == HALVES - 1 and first == 0:
                 columns = slice(0, 2 * HID)
@@ -298,27 +304,21 @@ def tile_treelstmcellv2_t_kernel(
                 out=out_view[g][:, tiles, columns], in_=result[g][:, tiles, columns]
             )
 
-        def copy_c(step, tiles=ALL_TILES):
+        def copy_c(step):
             if step % HALVES == 0:
                 result[step // HALVES] = stores.tile([P, TILES, 2 * HID], F32, name="result")
-            nc.vector.tensor_copy(
-                out=c_columns(step)[:, tiles], in_=cell_back[step][:, tiles]
-            )
-            store(step, HID, tiles)
+            nc.vector.tensor_copy(out=c_columns(step), in_=cell_back[step][:])
+            store(step, HID, ALL_TILES)
 
-        def tanh(step, tiles=ALL_TILES):
-            if step not in tanh_c:
-                tanh_c[step] = gates.tile([P, TILES, P], F32, name="tanh_c")
-            nc.scalar.activation(
-                out=tanh_c[step][:, tiles], in_=cell_back[step][:, tiles], func=ACT.Tanh
-            )
+        def tanh(step):
+            tanh_c[step] = gates.tile([P, TILES, P], F32, name="tanh_c")
+            nc.scalar.activation(out=tanh_c[step][:], in_=cell_back[step][:], func=ACT.Tanh)
 
-        def make_h(step, tiles=ALL_TILES):
+        def make_h(step):
             nc.vector.tensor_tensor(
-                out=h_columns(step)[:, tiles], in0=tanh_c[step][:, tiles],
-                in1=o_back[step][:, tiles], op=ALU.mult,
+                out=h_columns(step), in0=tanh_c[step][:], in1=o_back[step][:], op=ALU.mult
             )
-            store(step, 0, tiles)
+            store(step, 0, ALL_TILES)
 
         def make_fresh(step):
             if 0 <= step < STEPS:
@@ -358,28 +358,28 @@ def tile_treelstmcellv2_t_kernel(
         turn(2, "turned")
         quantise(w_unit[U])
         multiply(0, U)
-        regroup(w_unit[O], nc.vector.tensor_copy, 0, UNIT_ROWS)
+        regroup(w_unit[O], nc.scalar.copy, 0, UNIT_ROWS)
+        combine(3)
         activate(0, I)
         multiply(1, F)
-        combine(3)
-        sum_children(0)
-        activate(0, U)
-        turn(3, "cell_back")
         quantise(w_unit[O])
+        activate(0, U)
         multiply(0, O)
+        sum_children(0)
+        turn(3, "cell_back")
         multiply(1, I)
-        regroup(2, nc.scalar.copy, 0, UNIT_ROWS)
+        regroup(2, nc.vector.tensor_copy, 0, UNIT_ROWS)
         make_kept(0)
         make_fresh(0)
-        add_terms(0)
-        regroup(3, nc.vector.tensor_copy, 0, UNIT_ROWS)
         activate(0, O)
+        regroup(3, nc.scalar.copy, 0, UNIT_ROWS)
         sum_children(1)
         quantise(2)
         multiply(1, U)
-        multiply(1, O)
         combine(4)
+        multiply(1, O)
         quantise(3)
+        add_terms(0)
 
         for p in range(1, STEPS):
             unit = p + LEAD
@@ -408,10 +408,30 @@ def tile_treelstmcellv2_t_kernel(
             quantise(unit - 1)
 
         last = STEPS - 1
-        turn_back(last, "acc%d" % I)
-        turn_o(last, "acc%d" % U)
-        for first in range(0, TILES, TILES // 2):
-            tiles = slice(first, first + TILES // 2)
-            tanh(last, tiles)
-            copy_c(last, tiles)
-            make_h(last, tiles)
+        middle = TILES // 2
+        parts = (slice(0, middle), slice(middle, TILES))
+        cells = [
+            psum.tile([P, middle, P], F32, name="cell", tag="acc%d" % position)
+            for position in (F, I)
+        ]
+        opened = [
+            psum.tile([P, middle, P], F32, name="opened", tag="acc%d" % position)
+            for position in (U, O)
+        ]
+        tanh_c[last] = gates.tile([P, TILES, P], F32, name="tanh_c")
+        for cell, tiles in zip(cells, parts):
+            turn_terms(last, cell, tiles.start, tiles.stop)
+        for bank, tiles in zip(opened, parts):
+            turn_gate_o(last, bank, tiles.start, tiles.stop)
+        for cell, tiles in zip(cells, parts):
+            nc.scalar.activation(out=tanh_c[last][:, tiles], in_=cell[:], func=ACT.Tanh)
+        for cell, bank, tiles, copy in zip(
+            cells, opened, parts, (nc.vector.tensor_copy, nc.scalar.copy)
+        ):
+            copy(out=c_columns(last)[:, tiles], in_=cell[:])
+            store(last, HID, tiles)
+            nc.vector.tensor_tensor(
+                out=h_columns(last)[:, tiles], in0=tanh_c[last][:, tiles], in1=bank[:],
+                op=ALU.mult,
+            )
+            store(last, 0, tiles)

from contextlib import ExitStack

import concourse.mybir as mybir
from concourse.masks import make_identity

F32 = mybir.dt.float32
BF16 = mybir.dt.bfloat16
U32 = mybir.dt.uint32
U8 = mybir.dt.uint8
FP8X4 = mybir.dt.float8_e4m3fn_x4
ACT = mybir.ActivationFunctionType
ALU = mybir.AluOpType

P = 128
PACK = 4
NODES = 8192
CHILDREN = 2
HID = 256
K_IN = 2 * HID
GROUP = 512
TILES = GROUP // P
N_GROUPS = NODES // GROUP
HALVES = HID // P
STEPS = N_GROUPS * HALVES
PAIR_NODES = P // CHILDREN
PAIR_TILES = GROUP // PAIR_NODES
PAIR_PLACES = PAIR_NODES // TILES

ALL_TILES = slice(0, TILES)
PAIRED_TILES = 3
UNIT_TILES = 2
UNIT_ROWS = UNIT_TILES * P
GROUP_UNITS = GROUP // UNIT_ROWS
HC_UNITS = N_GROUPS * GROUP_UNITS
W_TILES = 4 * HALVES
W_UNITS = W_TILES // UNIT_TILES
F_TILE = 3 * HALVES

GATES = (
    (0 * HALVES, ACT.Sigmoid),
    (2 * HALVES, ACT.Tanh),
    (F_TILE, ACT.Sigmoid),
    (1 * HALVES, ACT.Sigmoid),
)
I, U, F, O = 0, 1, 2, 3
LEAD = 4
VECTOR_ROWS = 144
LOAD_BUFS = 4

FLOPS = 2 * NODES * K_IN * 4 * HID


def tile_treelstmcellv2_t_kernel(
    tc, mailbox_h, mailbox_c, U_iou_w, b_iou, U_f_w, U_f_b, out
):
    nc = tc.nc
    h_view = mailbox_h.rearrange("(g p j) k f -> g p j k f", j=TILES, p=P)
    out_view = out.rearrange("(g p j) c -> g p j c", j=TILES, p=P)
    c_view = mailbox_c.rearrange("n k f -> (n k) f").rearrange(
        "(g r p) f -> g p r f", r=PAIR_TILES, p=P
    )

    with ExitStack() as ctx:
        const = ctx.enter_context(tc.tile_pool(name="const", bufs=1))
        loads = ctx.enter_context(tc.tile_pool(name="loads", bufs=LOAD_BUFS))
        units = ctx.enter_context(tc.tile_pool(name="units", bufs=4))
        codes = ctx.enter_context(tc.tile_pool(name="codes", bufs=4))
        gates = ctx.enter_context(tc.tile_pool(name="gates", bufs=2))
        stores = ctx.enter_context(tc.tile_pool(name="stores", bufs=3))
        psum = ctx.enter_context(tc.psum_pool(name="psum", bufs=1))
        ctx.enter_context(tc.manual_schedule())

        h_rows, c_rows, unit_pairs, turned, grouped = {}, {}, {}, {}, {}
        hc_codes, hc_scales, acc, gate, c_sum = {}, {}, {}, {}, {}
        added = {}
        fresh, kept, cell_back, o_back, tanh_c, result = {}, {}, {}, {}, {}, {}

        def load_h(g, pieces):
            h_rows[g] = loads.tile([P, TILES, CHILDREN, HID], BF16, name="h_rows")
            width = TILES // pieces
            for first in range(0, TILES, width):
                tiles = slice(first, first + width)
                nc.sync.dma_start(out=h_rows[g][:, tiles], in_=h_view[g][:, tiles])

        def load_c(g):
            c_rows[g] = loads.tile([P, PAIR_TILES, HID], BF16, name="c_rows")
            nc.sync.dma_start(out=c_rows[g][:], in_=c_view[g])

        def load(g):
            if g < N_GROUPS:
                load_h(g, 1)
                load_c(g)

        bias_rows = const.tile([P, P], BF16)
        nc.vector.memset(bias_rows[:], 0.0)
        w_rows = const.tile([P, W_TILES, K_IN], BF16)
        w_tiles_iou = U_iou_w.rearrange("(m p) k -> p m k", p=P)
        w_tiles_f = U_f_w.rearrange("(m p) k -> p m k", p=P)
        nc.sync.dma_start(out=w_rows[:, F_TILE:W_TILES, :], in_=w_tiles_f)
        load_h(0, GROUP_UNITS)
        nc.sync.dma_start(
            out=bias_rows[0:F_TILE, :], in_=b_iou.rearrange("o (m c) -> (o m) c", c=P)
        )
        nc.sync.dma_start(
            out=bias_rows[F_TILE:W_TILES, :], in_=U_f_b.rearrange("(m c) -> m c", c=P)
        )
        for position in (I, U, O):
            m = GATES[position][0]
            nc.sync.dma_start(
                out=w_rows[:, m : m + UNIT_TILES, :], in_=w_tiles_iou[:, m : m + UNIT_TILES, :]
            )
        load_h(1, GROUP_UNITS)
        load_c(0)
        for g in range(2, LOAD_BUFS):
            load_h(g, 1)
            load_c(g - 1)
        load_c(LOAD_BUFS - 1)

        table_in = const.tile([P, 1], F32)
        nc.gpsimd.memset(table_in[:], 0.0)
        table_out = const.tile([P, 1], F32)
        nc.scalar.activation(out=table_out[:], in_=table_in[:], func=ACT.Sigmoid)

        ident_bf = const.tile([P, P], BF16)
        make_identity(nc, ident_bf[:])
        ident_f32 = const.tile([P, P], F32)
        make_identity(nc, ident_f32[:])
        pair_sum = const.tile([P, TILES, PAIR_PLACES], BF16)
        ident_pairs = ident_bf[:].rearrange(
            "p (s j two) -> p two j s", j=TILES, two=CHILDREN
        )
        nc.vector.tensor_tensor(
            out=pair_sum[:], in0=ident_pairs[:, 0], in1=ident_pairs[:, 1], op=ALU.add
        )

        w_codes = const.tile([P, W_TILES * P], U32, align_bytes=64)
        w_scales = const.tile([P, W_TILES * P], U8, align_bytes=64)
        for unit in range(-W_UNITS, 0):
            first = (unit + W_UNITS) * UNIT_TILES
            unit_pairs[unit] = w_rows[:].bitcast(F32)[:, first : first + UNIT_TILES, :]

        def combine(unit):
            if not 0 <= unit < HC_UNITS:
                return
            g, part = divmod(unit, GROUP_UNITS)
            rows = h_rows[g][:, part * UNIT_TILES : (part + 1) * UNIT_TILES, :, :]
            hc = units.tile([P, UNIT_TILES, K_IN], BF16, name="hc")
            nc.vector.tensor_tensor(
                out=hc[:, :, 0:HID], in0=rows[:, :, 0, :], in1=rows[:, :, 1, :], op=ALU.add
            )
            nc.vector.tensor_tensor(
                out=hc[:, :, HID:K_IN], in0=rows[:, :, 0, :], in1=rows[:, :, 1, :], op=ALU.max
            )
            unit_pairs[unit] = hc[:].bitcast(F32)

        def turn(unit, bank):
            if not -W_UNITS <= unit < HC_UNITS:
                return
            turned[unit] = psum.tile([P, PACK // 2, UNIT_ROWS], F32, name="turned", tag=bank)
            for r in range(UNIT_TILES):
                for v in range(PACK // 2):
                    nc.tensor.transpose(
                        turned[unit][:, v, r * P : (r + 1) * P],
                        unit_pairs[unit][:, r, v * P : (v + 1) * P],
                        ident_f32[:],
                    )

        def regroup(unit, copy, first, last):
            if not -W_UNITS <= unit < HC_UNITS or first == last:
                return
            if unit not in grouped:
                grouped[unit] = units.tile(
                    [P, UNIT_ROWS, PACK], BF16, name="grouped", align_bytes=64
                )
            copy(
                out=grouped[unit][:].bitcast(F32)[:, first:last, :],
                in_=turned[unit][:, :, first:last].rearrange("p v r -> p r v"),
            )

        def quantise(unit):
            if not -W_UNITS <= unit < HC_UNITS:
                return
            g, part = divmod(unit, GROUP_UNITS)
            if unit >= 0 and part == 0:
                hc_codes[g] = codes.tile([P, GROUP], U32, name="hc_codes", align_bytes=64)
                hc_scales[g] = codes.tile([P, GROUP], U8, name="hc_scales", align_bytes=64)
            if unit < 0:
                words, scales, first = w_codes, w_scales, (unit + W_UNITS) * UNIT_ROWS
            else:
                words, scales, first = hc_codes[g], hc_scales[g], part * UNIT_ROWS
            nc.vector.quantize_mx(
                out=words[:, first : first + UNIT_ROWS].bitcast(FP8X4),
                scales=scales[:, first : first + UNIT_ROWS],
                in_=grouped[unit][:].rearrange("p r t -> p (r t)"),
            )

        def multiply(step, position):
            if not 0 <= step < STEPS:
                return
            g, half = divmod(step, HALVES)
            m = GATES[position][0] + half
            acc[step, position] = psum.tile([P, GROUP], F32, name="acc", tag="acc%d" % position)
            nc.tensor.matmul_mx(
                out=acc[step, position][:],
                lhsT=w_codes[:, m * P : (m + 1) * P].bitcast(FP8X4),
                lhsT_scale=w_scales[:, m * P : (m + 1) * P],
                rhs=hc_codes[g][:].bitcast(FP8X4),
                rhs_scale=hc_scales[g][:],
                start=True,
                stop=True,
            )

        def activate(step, position):
            if not 0 <= step < STEPS:
                return
            first_tile, func = GATES[position]
            m = first_tile + step % HALVES
            gate[step, position] = gates.tile([P, GROUP], F32, name="gate%d" % position)
            nc.scalar.activation(
                out=gate[step, position][:], in_=acc[step, position][:], func=func,
                bias=bias[:, m : m + 1], scale=1.0,
            )

        def product(engine, name, in0, in1):
            value = gates.tile([P, GROUP], F32, name=name)
            engine.tensor_tensor(out=value[:], in0=in0, in1=in1, op=ALU.mult)
            return value

        def sum_children(step):
            if not 0 <= step < STEPS:
                return
            g, half = divmod(step, HALVES)
            c_sum[step] = psum.tile([P, TILES, P], F32, name="c_sum")
            for r in range(PAIR_TILES):
                nc.tensor.matmul(
                    out=c_sum[step][:, :, r * PAIR_PLACES : (r + 1) * PAIR_PLACES],
                    lhsT=c_rows[g][:, r, half * P : (half + 1) * P],
                    rhs=pair_sum[:],
                    start=True,
                    stop=True,
                )
            if half == HALVES - 1:
                load(g + LOAD_BUFS)

        def turn_terms(step, bank, first, last):
            for j in range(first, last):
                nodes = slice(j * P, (j + 1) * P)
                nc.tensor.matmul(
                    out=bank[:, j - first, :], lhsT=fresh[step][:, nodes], rhs=ident_f32[:],
                    is_transpose=True, start=True, stop=False,
                )
                nc.tensor.matmul(
                    out=bank[:, j - first, :], lhsT=kept[step][:, nodes], rhs=ident_f32[:],
                    is_transpose=True, start=False, stop=True,
                )

        def turn_gate_o(step, bank, first, last):
            for j in range(first, last):
                nc.tensor.transpose(
                    bank[:, j - first, :], gate[step, O][:, j * P : (j + 1) * P], ident_f32[:]
                )

        def turn_back(step):
            cell_back[step] = psum.tile([P, TILES, P], F32, name="cell_back")
            turn_terms(step, cell_back[step], 0, PAIRED_TILES)

        def add_terms(step):
            if step == STEPS - 1:
                return
            added[step] = gates.tile([P, (TILES - PAIRED_TILES) * P], F32, name="added")
            nodes = slice(PAIRED_TILES * P, GROUP)
            nc.vector.tensor_tensor(
                out=added[step][:], in0=fresh[step][:, nodes], in1=kept[step][:, nodes], op=ALU.add
            )

        def turn_sum_back(step):
            for j in range(PAIRED_TILES, TILES):
                nodes = slice((j - PAIRED_TILES) * P, (j - PAIRED_TILES + 1) * P)
                nc.tensor.transpose(
                    cell_back[step][:, j, :], added[step][:, nodes], ident_f32[:]
                )

        def turn_o(step):
            o_back[step] = psum.tile([P, TILES, P], F32, name="o_back")
            turn_gate_o(step, o_back[step], 0, TILES)

        def c_columns(step):
            g, half = divmod(step, HALVES)
            return result[g][:, :, HID + half * P : HID + (half + 1) * P]

        def h_columns(step):
            g, half = divmod(step, HALVES)
            return result[g][:, :, half * P : (half + 1) * P]

        def store(step, first, tiles):
            g, half = divmod(step, HALVES)
            if g >= N_GROUPS - 2:
                columns = slice(first + half * P, first + (half + 1) * P)
            elif half == HALVES - 1 and first == 0:
                columns = slice(0, 2 * HID)
            else:
                return
            nc.sync.dma_start(
                out=out_view[g][:, tiles, columns], in_=result[g][:, tiles, columns]
            )

        def copy_c(step):
            if step % HALVES == 0:
                result[step // HALVES] = stores.tile([P, TILES, 2 * HID], F32, name="result")
            nc.vector.tensor_copy(out=c_columns(step), in_=cell_back[step][:])
            store(step, HID, ALL_TILES)

        def tanh(step):
            tanh_c[step] = gates.tile([P, TILES, P], F32, name="tanh_c")
            nc.scalar.activation(out=tanh_c[step][:], in_=cell_back[step][:], func=ACT.Tanh)

        def make_h(step):
            nc.vector.tensor_tensor(
                out=h_columns(step), in0=tanh_c[step][:], in1=o_back[step][:], op=ALU.mult
            )
            store(step, 0, ALL_TILES)

        def make_fresh(step):
            if 0 <= step < STEPS:
                engine = nc.vector if step == STEPS - 1 else nc.gpsimd
                fresh[step] = product(engine, "fresh", gate[step, I][:], gate[step, U][:])

        def make_kept(step):
            if 0 <= step < STEPS:
                kept[step] = product(nc.vector, "kept", gate[step, F][:], c_sum[step][:].rearrange("p j n -> p (j n)"))

        w_unit = {position: GATES[position][0] // UNIT_TILES - W_UNITS for position in (I, U, F, O)}
        turn(w_unit[F], "acc%d" % O)
        regroup(w_unit[F], nc.scalar.copy, 0, UNIT_ROWS)
        combine(0)
        turn(0, "acc%d" % U)
        regroup(0, nc.scalar.copy, 0, UNIT_ROWS)
        combine(1)
        quantise(w_unit[F])
        turn(1, "acc%d" % I)
        regroup(1, nc.scalar.copy, 0, UNIT_ROWS)
        quantise(0)
        turn(w_unit[I], "turned")
        regroup(w_unit[I], nc.scalar.copy, 0, UNIT_ROWS)
        bias_turned = psum.tile([P, P], BF16, tag="c_sum")
        nc.tensor.transpose(bias_turned[:], bias_rows[:], ident_bf[:])
        bias = const.tile([P, W_TILES], F32)
        nc.vector.tensor_copy(out=bias[:], in_=bias_turned[:, 0:W_TILES])
        turn(w_unit[U], "cell_back")
        quantise(1)
        multiply(0, F)
        turn(w_unit[O], "o_back")
        quantise(w_unit[I])
        multiply(0, I)
        regroup(w_unit[U], nc.scalar.copy, 0, UNIT_ROWS)
        combine(2)
        activate(0, F)
        turn(2, "turned")
        quantise(w_unit[U])
        multiply(0, U)
        regroup(w_unit[O], nc.scalar.copy, 0, UNIT_ROWS)
        combine(3)
        activate(0, I)
        multiply(1, F)
        quantise(w_unit[O])
        activate(0, U)
        multiply(0, O)
        sum_children(0)
        turn(3, "cell_back")
        multiply(1, I)
        regroup(2, nc.vector.tensor_copy, 0, UNIT_ROWS)
        make_kept(0)
        make_fresh(0)
        activate(0, O)
        regroup(3, nc.scalar.copy, 0, UNIT_ROWS)
        sum_children(1)
        quantise(2)
        multiply(1, U)
        combine(4)
        multiply(1, O)
        quantise(3)
        add_terms(0)

        for p in range(1, STEPS):
            unit = p + LEAD
            turn_back(p - 1)
            turn_sum_back(p - 1)
            turn(unit - 1, "turned")
            turn_o(p - 1)
            activate(p, F)
            multiply(p + 1, F)
            combine(unit)
            make_kept(p)
            activate(p, I)
            multiply(p + 1, I)
            activate(p, U)
            multiply(p + 1, U)
            make_fresh(p)
            regroup(unit - 1, nc.vector.tensor_copy, 0, VECTOR_ROWS)
            tanh(p - 1)
            copy_c(p - 1)
            activate(p, O)
            multiply(p + 1, O)
            sum_children(p + 1)
            make_h(p - 1)
            add_terms(p)
            regroup(unit - 1, nc.scalar.copy, VECTOR_ROWS, UNIT_ROWS)
            quantise(unit - 1)

        last = STEPS - 1
        middle = TILES // 2
        parts = (slice(0, middle), slice(middle, TILES))
        cells = [
            psum.tile([P, middle, P], F32, name="cell", tag="acc%d" % position)
            for position in (F, I)
        ]
        opened = [
            psum.tile([P, middle, P], F32, name="opened", tag="acc%d" % position)
            for position in (U, O)
        ]
        tanh_c[last] = gates.tile([P, TILES, P], F32, name="tanh_c")
        for cell, tiles in zip(cells, parts):
            turn_terms(last, cell, tiles.start, tiles.stop)
        for bank, tiles in zip(opened, parts):
            turn_gate_o(last, bank, tiles.start, tiles.stop)
        for cell, tiles in zip(cells, parts):
            nc.scalar.activation(out=tanh_c[last][:, tiles], in_=cell[:], func=ACT.Tanh)
        for cell, bank, tiles, copy in zip(
            cells, opened, parts, (nc.vector.tensor_copy, nc.scalar.copy)
        ):
            copy(out=c_columns(last)[:, tiles], in_=cell[:])
            store(last, HID, tiles)
            nc.vector.tensor_tensor(
                out=h_columns(last)[:, tiles], in0=tanh_c[last][:, tiles], in1=bank[:],
                op=ALU.mult,
            )
            store(last, 0, tiles)
